import numpy as np
import ml_dtypes


def mxq(x, axis, fmt="e4m3"):
    dtype, down = {"e4m3": (ml_dtypes.float8_e4m3fn, 7), "e5m2": (ml_dtypes.float8_e5m2, 14)}[fmt]
    v = np.moveaxis(np.asarray(x, np.float32).astype(ml_dtypes.bfloat16).astype(np.float64), axis, -1)
    blocks = v.reshape(v.shape[:-1] + (-1, 32))
    amax = np.abs(blocks).max(-1, keepdims=True)
    byte = np.maximum(np.where(amax > 0, np.frexp(amax)[1] - 1 + 127, 0) - down, 1)
    scale = np.exp2(byte - 127.0)
    codes = (blocks / scale).astype(np.float32).astype(dtype).astype(np.float64)
    return np.moveaxis((codes * scale).reshape(v.shape), -1, axis)


WIDE = False


def mx_kscale(k):
    if not WIDE:
        return np.ones(k)
    levels = np.array([10, -10, 5, -5, 0])
    if k % 512:
        return np.exp2(np.random.permutation(np.resize(levels, k // 32))).repeat(32)
    a = np.empty((k // 512, 16))
    for p in range(k // 512):
        a[p, :8] = np.random.permutation(np.resize(levels, 8))
        for g in range(8):
            far = levels[np.abs(levels - a[p, g]) >= 10]
            a[p, g + 8] = far[np.random.randint(len(far))]
    return np.exp2(a.ravel()).repeat(32)


BF16 = ml_dtypes.bfloat16


def bf(x):
    return np.asarray(x, np.float32).astype(BF16)


def f64(x):
    return np.asarray(x).astype(np.float64)


B, D = 8192, 512
C = 8.0


def sigmoid(v):
    return 1.0 / (1.0 + np.exp(-v))


def softplus(v):
    return np.logaddexp(v, 0.0)


def setup_inputs():
    s = mx_kscale(D)
    xt = bf(np.random.standard_normal((B, D)) * s)
    ht_minus_1 = bf(np.random.standard_normal((B, D)) * s)
    Wa = bf(np.random.standard_normal((D, D)) / np.sqrt(D) / s[None, :])
    Wx = bf(np.random.standard_normal((D, D)) / np.sqrt(D) / s[None, :])
    ba = bf(np.random.standard_normal((1, D)) * 0.1)
    bx = bf(np.random.standard_normal((1, D)) * 0.1)
    Lambda = bf(np.random.uniform(-3.0, -1.0, (1, D)))
    return {"xt": xt, "ht_minus_1": ht_minus_1, "Wa": Wa, "Wx": Wx, "ba": ba, "bx": bx, "Lambda": Lambda}


def reference(xt, ht_minus_1, Wa, Wx, ba, bx, Lambda):
    x = f64(xt)
    xq = mxq(x, 1, "e4m3")
    rt = sigmoid((xq @ mxq(f64(Wa), 1, "e4m3").T) + f64(ba))
    it = sigmoid((xq @ mxq(f64(Wx), 1, "e4m3").T) + f64(bx))
    log_at = -(C * softplus(f64(Lambda))) * rt
    at = np.exp(log_at)
    ht = at * f64(ht_minus_1) + np.sqrt(1.0 - at ** 2) * (it * x)
    return ht

@@ -1,0 +1,372 @@
+from contextlib import ExitStack
+
+import concourse.mybir as mybir
+from concourse.masks import make_identity
+
+FLOPS = 2 * 2 * 8192 * 512 * 512
+
+F32 = mybir.dt.float32
+BF16 = mybir.dt.bfloat16
+U32 = mybir.dt.uint32
+U8 = mybir.dt.uint8
+FP8X4 = mybir.dt.float8_e4m3fn_x4
+ACT = mybir.ActivationFunctionType
+ALU = mybir.AluOpType
+
+P = 128
+D = 512
+GB = 512
+NG = 16
+W4 = 4 * GB
+CHUNKS = (4, 4, 4, 4)
+NT = 4
+LX = 3
+LH = 2
+MX_POS = 2
+EARLY_F = {14: 12, 15: 13}
+
+
+def tile_cell_t_kernel(tc, xt, ht_minus_1, Wa, Wx, ba, bx, Lambda, out):
+    nc = tc.nc
+    x_v = xt.rearrange("(g p j) k -> g p (j k)", p=P, j=4)
+    h_v = ht_minus_1.rearrange("(g p j) k -> g p (j k)", p=P, j=4)
+    o_v = out.rearrange("(g p j) k -> g p (j k)", p=P, j=4)
+    o_v4 = out.rearrange("(g p j) k -> g p j k", p=P, j=4)
+
+    with ExitStack() as ctx:
+        const = ctx.enter_context(tc.tile_pool(name="const", bufs=1))
+        xpool = ctx.enter_context(tc.tile_pool(name="xpool", bufs=max(CHUNKS) + LX))
+        hpool = ctx.enter_context(tc.tile_pool(name="hpool", bufs=4))
+        gpool = ctx.enter_context(tc.tile_pool(name="gpool", bufs=2))
+        cpool = ctx.enter_context(tc.tile_pool(name="cpool", bufs=3))
+        tapool = ctx.enter_context(tc.tile_pool(name="tapool", bufs=1))
+        ppool = ctx.enter_context(tc.tile_pool(name="ppool", bufs=max(CHUNKS) + 1))
+        apool = ctx.enter_context(tc.tile_pool(name="apool", bufs=max(CHUNKS) + 1))
+        rpool = ctx.enter_context(tc.tile_pool(name="rpool", bufs=max(CHUNKS) + 1))
+        psum = ctx.enter_context(tc.psum_pool(name="psum", bufs=1))
+        ctx.enter_context(tc.manual_schedule())
+
+        tcount = [0]
+
+        def tbank():
+            i = tcount[0]
+            tcount[0] = i + 1
+            return psum.tile([P, 512], F32, tag="T%d" % (i % NT), name="T_%d" % i)
+
+        xs, hs, grps, codes, scales, zs = {}, {}, {}, {}, {}, {}
+        tas, ps, a2s, rs = {}, {}, {}, {}
+
+        ident = const.tile([P, P], F32, name="ident")
+        make_identity(nc, ident[:])
+        vt = const.tile([P, P], F32, name="vt")
+        nc.vector.memset(vt[:], 0.0)
+        one = const.tile([P, 1], F32, name="one")
+        nc.vector.memset(one[:], 1.0)
+        quarter = const.tile([P, 1], F32, name="quarter")
+        nc.vector.memset(quarter[:], 0.25)
+        vt_bf = vt[:].bitcast(BF16)
+        for v, vec in enumerate((ba, bx, Lambda)):
+            nc.scalar.dma_start(out=vt_bf[2 * v:2 * v + 2, :],
+                                in_=vec.rearrange("o (u w) -> (o u) w", u=2))
+
+        def load_x(g):
+            xs[g] = xpool.tile([P, W4], BF16, tag="x", name="x%d" % g)
+            nc.sync.dma_start(out=xs[g][:], in_=x_v[g])
+
+        def load_h(g):
+            hs[g] = hpool.tile([P, W4], BF16, tag="h", name="h%d" % g)
+            nc.sync.dma_start(out=hs[g][:], in_=h_v[g])
+
+        def load_w(u, eng):
+            t = xpool.tile([P, W4], BF16, tag="x", name="w_sb%d" % u)
+            for i, w in enumerate((Wa, Wx)):
+                eng.dma_start(out=t[:, i * 1024:(i + 1) * 1024],
+                              in_=w[256 * u:256 * (u + 1), :].rearrange("(m e) k -> m (e k)", e=2))
+            return t
+
+        load_x(0)
+        w_sb = [load_w(0, nc.scalar)]
+        w_sb.append(load_w(1, nc.sync))
+        load_x(1)
+        load_x(2)
+        load_h(0)
+        load_h(1)
+
+        def word_transposes(src, half):
+            sv = src[:].bitcast(F32)
+            bank = tbank()
+            for jl in range(2):
+                for u in range(2):
+                    col = (2 * half + jl) * 256 + u * 128
+                    nc.tensor.transpose(bank[:, u * 256 + jl * 128:u * 256 + jl * 128 + 128],
+                                        sv[:, col:col + 128], ident[:])
+            return bank
+
+        def quant_transposes(src, half):
+            sv = src[:].bitcast(F32)
+            bank = tbank()
+            for jl in range(2):
+                for u in range(2):
+                    col = (2 * half + jl) * 256
+                    nc.tensor.transpose(bank[:, u * 256 + jl * 128:u * 256 + jl * 128 + 128],
+                                        sv[:, col + u:col + 256:2], ident[:])
+            return bank
+
+        def regroup_half(src, grp, half):
+            bank = quant_transposes(src, half)
+            nc.vector.tensor_copy(
+                out=grp[:, half * 512:(half + 1) * 512].rearrange("p (c u) -> p c u", u=2),
+                in_=bank[:].rearrange("p (u c) -> p c u", u=2))
+
+        def new_grp(name):
+            return gpool.tile([P, 1024], F32, tag="grp", name="grp_" + name, align_bytes=64)
+
+        def quantise(grp, cod, sca):
+            nc.vector.quantize_mx(out=cod[:].bitcast(FP8X4), scales=sca[:],
+                                  in_=grp[:].bitcast(BF16))
+
+        def prep_x(g, half):
+            if half == 0:
+                grps[g] = new_grp("x%d" % g)
+            regroup_half(xs[g], grps[g], half)
+
+        def quant_x(g):
+            codes[g] = cpool.tile([P, GB], U32, tag="cod", name="cod%d" % g, align_bytes=64)
+            scales[g] = cpool.tile([P, GB], U8, tag="sca", name="sca%d" % g, align_bytes=64)
+            quantise(grps[g], codes[g], scales[g])
+
+        cbank = tbank()
+        nc.tensor.transpose(cbank[:, 0:P], vt[:], ident[:])
+        raw = const.tile([P, 12], F32, name="raw")
+        nc.vector.tensor_copy(out=raw[:], in_=cbank[:].bitcast(BF16)[:, 0:12])
+        hb = const.tile([P, 8], F32, name="hb")
+        nc.vector.tensor_scalar_mul(out=hb[:], in0=raw[:, 0:8], scalar1=0.5)
+        lam = raw[:, 8:12]
+        sp_a = const.tile([P, 4], F32, name="sp_a")
+        nc.scalar.activation(out=sp_a[:], in_=lam, func=ACT.Abs)
+        sp_e = const.tile([P, 4], F32, name="sp_e")
+        nc.scalar.activation(out=sp_e[:], in_=sp_a[:], func=ACT.Exp, scale=-1.0)
+        sp_l = const.tile([P, 4], F32, name="sp_l")
+        nc.scalar.activation(out=sp_l[:], in_=sp_e[:], func=ACT.Ln, bias=one[:])
+
+        wcod, wsca, wgrp = [], [], []
+        for u in range(2):
+            wcod.append(const.tile([P, D], U32, name="wcod%d" % u, align_bytes=64))
+            wsca.append(const.tile([P, D], U8, name="wsca%d" % u, align_bytes=64))
+        prep_x(0, 0)
+        prep_x(0, 1)
+        wgrp.append(new_grp("w0"))
+        regroup_half(w_sb[0], wgrp[0], 0)
+        regroup_half(w_sb[0], wgrp[0], 1)
+        quant_x(0)
+        quantise(wgrp[0], wcod[0], wsca[0])
+        sp = const.tile([P, 4], F32, name="sp")
+        nc4 = const.tile([P, 4], F32, name="nc4")
+
+        def mx(g, gate, u):
+            for e in range(2):
+                col = (2 * gate + e) * P
+                z = psum.tile([P, 512], F32, tag="Z%d" % (2 * gate + e),
+                              name="z%d_%d_%d" % (gate, g, 2 * u + e))
+                nc.tensor.matmul_mx(
+                    out=z[:],
+                    lhsT=wcod[u][:, col:col + P].bitcast(FP8X4),
+                    lhsT_scale=wsca[u][:, col:col + P],
+                    rhs=codes[g][:].bitcast(FP8X4),
+                    rhs_scale=scales[g][:],
+                    start=True, stop=True)
+                zs[(g, gate, 2 * u + e)] = z
+
+        def act_a(g, u):
+            if u == 0:
+                tas[g] = tapool.tile([P, W4], F32, tag="ta", name="ta%d" % g)
+            for blk in (2 * u, 2 * u + 1):
+                nc.scalar.activation(out=tas[g][:, blk * GB:(blk + 1) * GB], in_=zs[(g, 0, blk)][:],
+                                     func=ACT.Tanh, scale=0.5, bias=hb[:, blk:blk + 1])
+
+        def act_b(g, u):
+            if u == 0:
+                ps[g] = ppool.tile([P, W4], F32, tag="p", name="p%d" % g)
+            for blk in (2 * u, 2 * u + 1):
+                nc.scalar.activation(out=ps[g][:, blk * GB:(blk + 1) * GB], in_=zs[(g, 1, blk)][:],
+                                     func=ACT.Tanh, scale=0.5, bias=hb[:, 4 + blk:5 + blk])
+
+        def act_c(g, u):
+            if u == 0:
+                a2s[g] = apool.tile([P, W4], F32, tag="a2", name="a2_%d" % g)
+            for blk in (2 * u, 2 * u + 1):
+                nc.scalar.activation(out=a2s[g][:, blk * GB:(blk + 1) * GB],
+                                     in_=tas[g][:, blk * GB:(blk + 1) * GB],
+                                     func=ACT.Exp, scale=nc4[:, blk:blk + 1], bias=nc4[:, blk:blk + 1])
+
+        def back_transposes(src, jj):
+            bank = tbank()
+            for blk in range(4):
+                nc.tensor.transpose(bank[:, blk * P:(blk + 1) * P],
+                                    src[:, blk * GB + jj * P:blk * GB + (jj + 1) * P], ident[:])
+            return bank[:].rearrange("p (u e m) -> p u m e", u=2, e=2)
+
+        def nat(t, jj):
+            return t[:, jj * D:(jj + 1) * D].rearrange("p (u m e) -> p u m e", u=2, e=2)
+
+        def at_h(g, jj):
+            if jj == 0:
+                rs[g] = rpool.tile([P, W4], F32, tag="r", name="r%d" % g)
+            bv = back_transposes(a2s[g], jj)
+            nc.vector.tensor_tensor(out=nat(rs[g], jj), in0=bv, in1=nat(hs[g], jj), op=ALU.mult)
+
+        def square(g):
+            nc.gpsimd.tensor_tensor(out=a2s[g][:], in0=a2s[g][:], in1=a2s[g][:], op=ALU.mult)
+
+        def act_e(g):
+            nc.scalar.activation(out=a2s[g][:], in_=a2s[g][:], func=ACT.Sqrt, scale=-0.25,
+                                 bias=quarter[:])
+
+        def fmul(g, half):
+            pv = ps[g][:].rearrange("p (k n) -> p k n", k=4)
+            bv = word_transposes(xs[g], half)[:].bitcast(BF16)
+            for u in range(2):
+                io = pv[:, 2 * u:2 * u + 2, half * 256:(half + 1) * 256]
+                nc.vector.scalar_tensor_tensor(
+                    out=io, in0=io, scalar=1.0,
+                    in1=bv[:, u * 512:(u + 1) * 512].rearrange("p (c e) -> p e c", e=2),
+                    op0=ALU.add, op1=ALU.mult)
+
+        def gmul(g):
+            nc.gpsimd.tensor_tensor(out=ps[g][:], in0=ps[g][:], in1=a2s[g][:], op=ALU.mult)
+
+        def gmul_quarter(g, jj, eng):
+            pv = ps[g][:].rearrange("p (k n) -> p k n", k=4)[:, :, jj * P:(jj + 1) * P]
+            sv = a2s[g][:].rearrange("p (k n) -> p k n", k=4)[:, :, jj * P:(jj + 1) * P]
+            eng.tensor_tensor(out=pv, in0=pv, in1=sv, op=ALU.mult)
+
+        def square_aside(g):
+            nc.gpsimd.tensor_tensor(out=tas[g][:], in0=a2s[g][:], in1=a2s[g][:], op=ALU.mult)
+
+        def act_e_aside(g):
+            nc.scalar.activation(out=a2s[g][:], in_=tas[g][:], func=ACT.Sqrt, scale=-0.25,
+                                 bias=quarter[:])
+
+        def square_on_scalar(g):
+            nc.scalar.activation(out=a2s[g][:], in_=a2s[g][:], func=ACT.Square)
+
+        def store_quarter(g, jj):
+            nc.sync.dma_start(out=o_v4[g][:, jj, :], in_=rs[g][:, jj * D:(jj + 1) * D])
+
+        def finish(g, jj):
+            bv = back_transposes(ps[g], jj)
+            nc.vector.tensor_tensor(out=nat(rs[g], jj), in0=bv, in1=nat(rs[g], jj), op=ALU.add)
+
+        def store(g):
+            nc.sync.dma_start(out=o_v[g], in_=rs[g][:])
+
+        mx(0, 0, 0)
+        mx(0, 1, 0)
+        wgrp.append(new_grp("w1"))
+        regroup_half(w_sb[1], wgrp[1], 0)
+        regroup_half(w_sb[1], wgrp[1], 1)
+        nc.vector.scalar_tensor_tensor(out=sp[:], in0=lam, scalar=0.0, in1=sp_l[:],
+                                       op0=ALU.max, op1=ALU.add)
+        nc.vector.tensor_scalar_mul(out=nc4[:], in0=sp[:], scalar1=-4.0)
+        quantise(wgrp[1], wcod[1], wsca[1])
+        prep_x(1, 0)
+        prep_x(1, 1)
+        pending = []
+        g0 = 0
+        for ci, n in enumerate(CHUNKS):
+            chunk = list(range(g0, g0 + n))
+            g0 += n
+            last_chunk = ci == len(CHUNKS) - 1
+            for j, g in enumerate(chunk):
+                pg = pending[0] if pending else None
+                pending = pending[1:]
+                more_x = g + 2 < NG
+                banks = []
+                if j > 0:
+                    banks.extend([("R", g - 1, jj) for jj in range(4)])
+                if more_x:
+                    banks.extend([("K", g + 2, 0), ("K", g + 2, 1)])
+                if pg is not None:
+                    banks.extend([("O", pg, jj) for jj in range(4)])
+                if g in EARLY_F:
+                    banks.extend([("F", EARLY_F[g], 0), ("F", EARLY_F[g], 1)])
+                state = {"i": 0, "quant": not more_x}
+
+                def emit(count):
+                    for item in banks[state["i"]:state["i"] + count]:
+                        kind, gg, part = item
+                        if kind == "R":
+                            at_h(gg, part)
+                            if part == 3:
+                                square(gg)
+                        elif kind == "K":
+                            prep_x(gg, part)
+                        elif kind == "F":
+                            fmul(gg, part)
+                        else:
+                            finish(gg, part)
+                            if not state["quant"]:
+                                quant_x(g + 2)
+                                state["quant"] = True
+                    state["i"] = state["i"] + count
+
+                act_a(g, 0)
+                act_b(g, 0)
+                mx(g, 0, 1)
+                emit(1)
+                mx(g, 1, 1)
+                act_c(g, 0)
+                act_a(g, 1)
+                act_b(g, 1)
+                if g == 0:
+                    quant_x(1)
+                emit(4)
+                if j < n - 1:
+                    mx(g + 1, 0, 0)
+                emit(1)
+                if j < n - 1:
+                    mx(g + 1, 1, 0)
+                act_c(g, 1)
+                emit(len(banks))
+                if not state["quant"]:
+                    quant_x(g + 2)
+                if g + LX < NG:
+                    load_x(g + LX)
+                if g + LH < NG:
+                    load_h(g + LH)
+                if pg is not None:
+                    store(pg)
+            last = chunk[-1]
+            early = [EARLY_F[k] for k in EARLY_F]
+            if last_chunk:
+                for jj in range(4):
+                    at_h(last, jj)
+                for g in chunk:
+                    if g == last:
+                        square_on_scalar(g)
+                    act_e(g)
+                    if g not in early:
+                        fmul(g, 0)
+                        fmul(g, 1)
+                    for jj in range(4):
+                        gmul_quarter(g, jj, nc.gpsimd)
+            else:
+                square_aside(last)
+                for jj in range(4):
+                    at_h(last, jj)
+                for i, g in enumerate(chunk):
+                    if i == MX_POS:
+                        mx(last + 1, 0, 0)
+                        mx(last + 1, 1, 0)
+                    if g == last:
+                        act_e_aside(g)
+                    else:
+                        act_e(g)
+                    fmul(g, 0)
+                    fmul(g, 1)
+                    gmul(g)
+            pending = pending + chunk
+        for pg in pending:
+            for jj in range(4):
+                finish(pg, jj)
+                store_quarter(pg, jj)

@@ -18,12 +18,14 @@ D = 512
 GB = 512
 NG = 16
 W4 = 4 * GB
-CHUNKS = (4, 4, 4, 4)
+CHUNKS = (5, 5, 4, 2)
 NT = 4
-LX = 3
 LH = 2
+LF = 4
+LEAD = 7
 MX_POS = 2
-EARLY_F = {14: 12, 15: 13}
+SLOTS = (1, 4, 1)
+PREP = {0: (2, 3), 1: (4, 5), 2: (6, 7), 3: (8, 9), 4: (10, 11), 8: (12,), 9: (13,), 12: (14,), 13: (15,)}
 
 
 def tile_cell_t_kernel(tc, xt, ht_minus_1, Wa, Wx, ba, bx, Lambda, out):
@@ -35,13 +37,14 @@ def tile_cell_t_kernel(tc, xt, ht_minus_1, Wa, Wx, ba, bx, Lambda, out):
 
     with ExitStack() as ctx:
         const = ctx.enter_context(tc.tile_pool(name="const", bufs=1))
-        xpool = ctx.enter_context(tc.tile_pool(name="xpool", bufs=max(CHUNKS) + LX))
-        hpool = ctx.enter_context(tc.tile_pool(name="hpool", bufs=4))
+        xpool = ctx.enter_context(tc.tile_pool(name="xpool", bufs=5))
+        fpool = ctx.enter_context(tc.tile_pool(name="fpool", bufs=LF))
+        hpool = ctx.enter_context(tc.tile_pool(name="hpool", bufs=3))
         gpool = ctx.enter_context(tc.tile_pool(name="gpool", bufs=2))
-        cpool = ctx.enter_context(tc.tile_pool(name="cpool", bufs=3))
+        cpool = ctx.enter_context(tc.tile_pool(name="cpool", bufs=LEAD + 2))
         tapool = ctx.enter_context(tc.tile_pool(name="tapool", bufs=1))
         ppool = ctx.enter_context(tc.tile_pool(name="ppool", bufs=max(CHUNKS) + 1))
-        apool = ctx.enter_context(tc.tile_pool(name="apool", bufs=max(CHUNKS) + 1))
+        apool = ctx.enter_context(tc.tile_pool(name="apool", bufs=max(CHUNKS)))
         rpool = ctx.enter_context(tc.tile_pool(name="rpool", bufs=max(CHUNKS) + 1))
         psum = ctx.enter_context(tc.psum_pool(name="psum", bufs=1))
         ctx.enter_context(tc.manual_schedule())
@@ -53,7 +56,7 @@ def tile_cell_t_kernel(tc, xt, ht_minus_1, Wa, Wx, ba, bx, Lambda, out):
             tcount[0] = i + 1
             return psum.tile([P, 512], F32, tag="T%d" % (i % NT), name="T_%d" % i)
 
-        xs, hs, grps, codes, scales, zs = {}, {}, {}, {}, {}, {}
+        xs, fs, hs, grps, codes, scales, zs = {}, {}, {}, {}, {}, {}, {}
         tas, ps, a2s, rs = {}, {}, {}, {}
 
         ident = const.tile([P, P], F32, name="ident")
@@ -72,6 +75,10 @@ def tile_cell_t_kernel(tc, xt, ht_minus_1, Wa, Wx, ba, bx, Lambda, out):
         def load_x(g):
             xs[g] = xpool.tile([P, W4], BF16, tag="x", name="x%d" % g)
             nc.sync.dma_start(out=xs[g][:], in_=x_v[g])
+
+        def load_f(g):
+            fs[g] = fpool.tile([P, W4], BF16, tag="f", name="f%d" % g)
+            nc.sync.dma_start(out=fs[g][:], in_=x_v[g])
 
         def load_h(g):
             hs[g] = hpool.tile([P, W4], BF16, tag="h", name="h%d" % g)
@@ -224,7 +231,7 @@ def tile_cell_t_kernel(tc, xt, ht_minus_1, Wa, Wx, ba, bx, Lambda, out):
 
         def fmul(g, half):
             pv = ps[g][:].rearrange("p (k n) -> p k n", k=4)
-            bv = word_transposes(xs[g], half)[:].bitcast(BF16)
+            bv = word_transposes(fs[g], half)[:].bitcast(BF16)
             for u in range(2):
                 io = pv[:, 2 * u:2 * u + 2, half * 256:(half + 1) * 256]
                 nc.vector.scalar_tensor_tensor(
@@ -232,8 +239,11 @@ def tile_cell_t_kernel(tc, xt, ht_minus_1, Wa, Wx, ba, bx, Lambda, out):
                     in1=bv[:, u * 512:(u + 1) * 512].rearrange("p (c e) -> p e c", e=2),
                     op0=ALU.add, op1=ALU.mult)
 
-        def gmul(g):
-            nc.gpsimd.tensor_tensor(out=ps[g][:], in0=ps[g][:], in1=a2s[g][:], op=ALU.mult)
+        def gmul(g, eng, parts):
+            w = W4 // parts
+            for i in range(parts):
+                eng.tensor_tensor(out=ps[g][:, i * w:(i + 1) * w], in0=ps[g][:, i * w:(i + 1) * w],
+                                  in1=a2s[g][:, i * w:(i + 1) * w], op=ALU.mult)
 
         def gmul_quarter(g, jj, eng):
             pv = ps[g][:].rearrange("p (k n) -> p k n", k=4)[:, :, jj * P:(jj + 1) * P]
@@ -248,7 +258,7 @@ def tile_cell_t_kernel(tc, xt, ht_minus_1, Wa, Wx, ba, bx, Lambda, out):
                                  bias=quarter[:])
 
         def square_on_scalar(g):
-            nc.scalar.activation(out=a2s[g][:], in_=a2s[g][:], func=ACT.Square)
+            nc.scalar.activation(out=tas[g][:], in_=a2s[g][:], func=ACT.Square)
 
         def store_quarter(g, jj):
             nc.sync.dma_start(out=o_v4[g][:, jj, :], in_=rs[g][:, jj * D:(jj + 1) * D])
@@ -271,30 +281,43 @@ def tile_cell_t_kernel(tc, xt, ht_minus_1, Wa, Wx, ba, bx, Lambda, out):
         quantise(wgrp[1], wcod[1], wsca[1])
         prep_x(1, 0)
         prep_x(1, 1)
+        loaded = {"x": 3, "h": 2, "f": 0}
+        loaders = {"x": load_x, "h": load_h, "f": load_f}
+
+        def load_up_to(kind, g):
+            while loaded[kind] < NG and loaded[kind] <= g:
+                loaders[kind](loaded[kind])
+                loaded[kind] += 1
+
         pending = []
+        unquantised = [1]
+        prepared = 1
+        vector_gmul = None
         g0 = 0
         for ci, n in enumerate(CHUNKS):
             chunk = list(range(g0, g0 + n))
             g0 += n
             last_chunk = ci == len(CHUNKS) - 1
+            per_step = -(-len(pending) // n)
             for j, g in enumerate(chunk):
-                pg = pending[0] if pending else None
-                pending = pending[1:]
-                more_x = g + 2 < NG
+                now, pending = pending[:per_step], pending[per_step:]
                 banks = []
                 if j > 0:
                     banks.extend([("R", g - 1, jj) for jj in range(4)])
-                if more_x:
-                    banks.extend([("K", g + 2, 0), ("K", g + 2, 1)])
-                if pg is not None:
+                for pg in now:
                     banks.extend([("O", pg, jj) for jj in range(4)])
-                if g in EARLY_F:
-                    banks.extend([("F", EARLY_F[g], 0), ("F", EARLY_F[g], 1)])
-                state = {"i": 0, "quant": not more_x}
+                if last_chunk and j > 0:
+                    banks.extend([("F", g - 1, 0), ("F", g - 1, 1)])
+                for k in PREP.get(g, ()):
+                    banks.extend([("K", k, 0), ("K", k, 1)])
+                    prepared = k
+                load_up_to("x", prepared + 3)
+                load_up_to("h", g + LH - 1)
+                load_up_to("f", g if last_chunk else g - 1 if j > 0 else -1)
+                pos = [0]
 
                 def emit(count):
-                    for item in banks[state["i"]:state["i"] + count]:
-                        kind, gg, part = item
+                    for kind, gg, part in banks[pos[0]:pos[0] + count]:
                         if kind == "R":
                             at_h(gg, part)
                             if part == 3:
@@ -305,56 +328,60 @@ def tile_cell_t_kernel(tc, xt, ht_minus_1, Wa, Wx, ba, bx, Lambda, out):
                             fmul(gg, part)
                         else:
                             finish(gg, part)
-                            if not state["quant"]:
-                                quant_x(g + 2)
-                                state["quant"] = True
-                    state["i"] = state["i"] + count
+                        if kind == "K" and part == 1:
+                            unquantised.append(gg)
+                        elif kind == "K" and unquantised:
+                            quant_x(unquantised.pop(0))
+                    pos[0] += count
 
+                if unquantised and g > 0:
+                    quant_x(unquantised.pop(0))
+                if vector_gmul is not None:
+                    gmul(vector_gmul, nc.vector, 1)
+                    vector_gmul = None
                 act_a(g, 0)
                 act_b(g, 0)
+                if j == 0:
+                    emit(2)
                 mx(g, 0, 1)
-                emit(1)
+                emit(SLOTS[0])
                 mx(g, 1, 1)
                 act_c(g, 0)
                 act_a(g, 1)
                 act_b(g, 1)
-                if g == 0:
-                    quant_x(1)
-                emit(4)
+                emit(SLOTS[1])
                 if j < n - 1:
                     mx(g + 1, 0, 0)
-                emit(1)
+                emit(SLOTS[2])
                 if j < n - 1:
                     mx(g + 1, 1, 0)
                 act_c(g, 1)
                 emit(len(banks))
-                if not state["quant"]:
-                    quant_x(g + 2)
-                if g + LX < NG:
-                    load_x(g + LX)
-                if g + LH < NG:
-                    load_h(g + LH)
-                if pg is not None:
+                for pg in now:
                     store(pg)
             last = chunk[-1]
-            early = [EARLY_F[k] for k in EARLY_F]
             if last_chunk:
+                for g in chunk[:-1]:
+                    act_e(g)
+                square_on_scalar(last)
                 for jj in range(4):
                     at_h(last, jj)
+                act_e_aside(last)
+                fmul(last, 0)
+                fmul(last, 1)
                 for g in chunk:
-                    if g == last:
-                        square_on_scalar(g)
-                    act_e(g)
-                    if g not in early:
-                        fmul(g, 0)
-                        fmul(g, 1)
                     for jj in range(4):
                         gmul_quarter(g, jj, nc.gpsimd)
+                for g in chunk:
+                    for jj in range(4):
+                        finish(g, jj)
+                        store_quarter(g, jj)
             else:
                 square_aside(last)
                 for jj in range(4):
                     at_h(last, jj)
                 for i, g in enumerate(chunk):
+                    load_up_to("f", min(g + LF - 1, last))
                     if i == MX_POS:
                         mx(last + 1, 0, 0)
                         mx(last + 1, 1, 0)
@@ -364,9 +391,7 @@ def tile_cell_t_kernel(tc, xt, ht_minus_1, Wa, Wx, ba, bx, Lambda, out):
                         act_e(g)
                     fmul(g, 0)
                     fmul(g, 1)
-                    gmul(g)
+                    if g < last:
+                        gmul(g, nc.gpsimd, 2)
+                vector_gmul = last
             pending = pending + chunk
-        for pg in pending:
-            for jj in range(4):
-                finish(pg, jj)
-                store_quarter(pg, jj)

@@ -22,10 +22,11 @@ CHUNKS = (5, 5, 4, 2)
 NT = 4
 LH = 2
 LF = 4
-LEAD = 7
+LEAD = 9
+NOW_GMUL = (3, 3, 1)
 MX_POS = 2
-SLOTS = (1, 4, 1)
-PREP = {0: (2, 3), 1: (4, 5), 2: (6, 7), 3: (8, 9), 4: (10, 11), 8: (12,), 9: (13,), 12: (14,), 13: (15,)}
+SLOTS = (0, 4, 1)
+PREP = {0: (2, 3,), 1: (4, 5,), 2: (6, 7,), 3: (8, 9,), 4: (10, 11,), 5: (12,), 8: (13,), 10: (14, 15,)}
 
 
 def tile_cell_t_kernel(tc, xt, ht_minus_1, Wa, Wx, ba, bx, Lambda, out):
@@ -57,7 +58,7 @@ def tile_cell_t_kernel(tc, xt, ht_minus_1, Wa, Wx, ba, bx, Lambda, out):
             return psum.tile([P, 512], F32, tag="T%d" % (i % NT), name="T_%d" % i)
 
         xs, fs, hs, grps, codes, scales, zs = {}, {}, {}, {}, {}, {}, {}
-        tas, ps, a2s, rs = {}, {}, {}, {}
+        tas, ps, a2s, qs, rs = {}, {}, {}, {}, {}
 
         ident = const.tile([P, P], F32, name="ident")
         make_identity(nc, ident[:])
@@ -247,18 +248,20 @@ def tile_cell_t_kernel(tc, xt, ht_minus_1, Wa, Wx, ba, bx, Lambda, out):
 
         def gmul_quarter(g, jj, eng):
             pv = ps[g][:].rearrange("p (k n) -> p k n", k=4)[:, :, jj * P:(jj + 1) * P]
-            sv = a2s[g][:].rearrange("p (k n) -> p k n", k=4)[:, :, jj * P:(jj + 1) * P]
+            sv = qs.get(g, a2s[g])[:].rearrange("p (k n) -> p k n", k=4)[:, :, jj * P:(jj + 1) * P]
             eng.tensor_tensor(out=pv, in0=pv, in1=sv, op=ALU.mult)
 
-        def square_aside(g):
-            nc.gpsimd.tensor_tensor(out=tas[g][:], in0=a2s[g][:], in1=a2s[g][:], op=ALU.mult)
-
         def act_e_aside(g):
-            nc.scalar.activation(out=a2s[g][:], in_=tas[g][:], func=ACT.Sqrt, scale=-0.25,
+            nc.scalar.activation(out=qs[g][:], in_=qs[g][:], func=ACT.Sqrt, scale=-0.25,
                                  bias=quarter[:])
 
         def square_on_scalar(g):
-            nc.scalar.activation(out=tas[g][:], in_=a2s[g][:], func=ACT.Square)
+            qs[g] = apool.tile([P, W4], F32, tag="a2", name="q%d" % g)
+            nc.scalar.activation(out=qs[g][:], in_=a2s[g][:], func=ACT.Square)
+
+        def square_apart(g):
+            qs[g] = apool.tile([P, W4], F32, tag="a2", name="q%d" % g)
+            nc.gpsimd.tensor_tensor(out=qs[g][:], in0=a2s[g][:], in1=a2s[g][:], op=ALU.mult)
 
         def store_quarter(g, jj):
             nc.sync.dma_start(out=o_v4[g][:, jj, :], in_=rs[g][:, jj * D:(jj + 1) * D])
@@ -269,6 +272,15 @@ def tile_cell_t_kernel(tc, xt, ht_minus_1, Wa, Wx, ba, bx, Lambda, out):
 
         def store(g):
             nc.sync.dma_start(out=o_v[g], in_=rs[g][:])
+
+        seen_codes = const.tile([P, 1], U32, name="seen_codes")
+        seen_f = const.tile([P, 1], F32, name="seen_f")
+
+        def gpsimd_after_quant(g):
+            nc.gpsimd.tensor_copy(out=seen_codes[:], in_=codes[g][:, 0:1])
+
+        def gpsimd_after_gmul(g):
+            nc.gpsimd.tensor_copy(out=seen_f[:], in_=ps[g][:, W4 - 1:W4])
 
         mx(0, 0, 0)
         mx(0, 1, 0)
@@ -292,7 +304,7 @@ def tile_cell_t_kernel(tc, xt, ht_minus_1, Wa, Wx, ba, bx, Lambda, out):
         pending = []
         unquantised = [1]
         prepared = 1
-        vector_gmul = None
+        late_gmul = []
         g0 = 0
         for ci, n in enumerate(CHUNKS):
             chunk = list(range(g0, g0 + n))
@@ -301,13 +313,15 @@ def tile_cell_t_kernel(tc, xt, ht_minus_1, Wa, Wx, ba, bx, Lambda, out):
             per_step = -(-len(pending) // n)
             for j, g in enumerate(chunk):
                 now, pending = pending[:per_step], pending[per_step:]
+                if last_chunk and j == n - 1:
+                    now, pending = now[:1], now[1:]
                 banks = []
                 if j > 0:
                     banks.extend([("R", g - 1, jj) for jj in range(4)])
                 for pg in now:
                     banks.extend([("O", pg, jj) for jj in range(4)])
-                if last_chunk and j > 0:
-                    banks.extend([("F", g - 1, 0), ("F", g - 1, 1)])
+                if last_chunk and j < n - 1:
+                    banks.extend([("F", g, 0), ("F", g, 1)])
                 for k in PREP.get(g, ()):
                     banks.extend([("K", k, 0), ("K", k, 1)])
                     prepared = k
@@ -319,8 +333,11 @@ def tile_cell_t_kernel(tc, xt, ht_minus_1, Wa, Wx, ba, bx, Lambda, out):
                 def emit(count):
                     for kind, gg, part in banks[pos[0]:pos[0] + count]:
                         if kind == "R":
+                            if part == 0 and last_chunk:
+                                square_apart(gg)
+                                gmul(late_gmul.pop(0), nc.gpsimd, 1)
                             at_h(gg, part)
-                            if part == 3:
+                            if part == 3 and not last_chunk:
                                 square(gg)
                         elif kind == "K":
                             prep_x(gg, part)
@@ -330,15 +347,19 @@ def tile_cell_t_kernel(tc, xt, ht_minus_1, Wa, Wx, ba, bx, Lambda, out):
                             finish(gg, part)
                         if kind == "K" and part == 1:
                             unquantised.append(gg)
-                        elif kind == "K" and unquantised:
-                            quant_x(unquantised.pop(0))
                     pos[0] += count
 
-                if unquantised and g > 0:
-                    quant_x(unquantised.pop(0))
-                if vector_gmul is not None:
-                    gmul(vector_gmul, nc.vector, 1)
-                    vector_gmul = None
+                if unquantised:
+                    while unquantised:
+                        quant_x(unquantised[0])
+                        quantised = unquantised.pop(0)
+                    if g > 1:
+                        gpsimd_after_quant(quantised)
+                if last_chunk and j == 0:
+                    gmul(g - 1, nc.vector, 1)
+                    gpsimd_after_gmul(g - 1)
+                if late_gmul and not (last_chunk and j == 1):
+                    gmul(late_gmul.pop(0), nc.gpsimd, 1)
                 act_a(g, 0)
                 act_b(g, 0)
                 if j == 0:
@@ -362,36 +383,50 @@ def tile_cell_t_kernel(tc, xt, ht_minus_1, Wa, Wx, ba, bx, Lambda, out):
             last = chunk[-1]
             if last_chunk:
                 for g in chunk[:-1]:
-                    act_e(g)
+                    act_e_aside(g)
                 square_on_scalar(last)
+                act_e_aside(last)
                 for jj in range(4):
                     at_h(last, jj)
-                act_e_aside(last)
                 fmul(last, 0)
                 fmul(last, 1)
-                for g in chunk:
+                for pg in pending:
+                    for jj in range(4):
+                        finish(pg, jj)
+                    store(pg)
+                for g in chunk[:-1]:
                     for jj in range(4):
                         gmul_quarter(g, jj, nc.gpsimd)
-                for g in chunk:
+                for g in chunk[:-1]:
                     for jj in range(4):
                         finish(g, jj)
                         store_quarter(g, jj)
+                for jj in range(4):
+                    gmul_quarter(last, jj, nc.vector)
+                for jj in range(4):
+                    finish(last, jj)
+                    store_quarter(last, jj)
             else:
-                square_aside(last)
+                while unquantised:
+                    quant_x(unquantised[0])
+                    quantised = unquantised.pop(0)
+                    gpsimd_after_quant(quantised)
                 for jj in range(4):
                     at_h(last, jj)
+                square(last)
                 for i, g in enumerate(chunk):
                     load_up_to("f", min(g + LF - 1, last))
                     if i == MX_POS:
                         mx(last + 1, 0, 0)
                         mx(last + 1, 1, 0)
-                    if g == last:
-                        act_e_aside(g)
-                    else:
-                        act_e(g)
+                    act_e(g)
                     fmul(g, 0)
                     fmul(g, 1)
-                    if g < last:
-                        gmul(g, nc.gpsimd, 2)
-                vector_gmul = last
+                    if i < NOW_GMUL[ci]:
+                        gmul(g, nc.gpsimd, 1)
+                    else:
+                        late_gmul.append(g)
+                if ci == len(CHUNKS) - 2:
+                    late_gmul.pop()
+                    chunk = [chunk[0], last] + chunk[1:-1]
             pending = pending + chunk

@@ -23,7 +23,7 @@ NT = 4
 LH = 2
 LF = 4
 LEAD = 9
-NOW_GMUL = (3, 3, 1)
+NOW_GMUL = (3, 3, 3)
 MX_POS = 2
 SLOTS = (0, 4, 1)
 PREP = {0: (2, 3,), 1: (4, 5,), 2: (6, 7,), 3: (8, 9,), 4: (10, 11,), 5: (12,), 8: (13,), 10: (14, 15,)}
@@ -60,12 +60,10 @@ def tile_cell_t_kernel(tc, xt, ht_minus_1, Wa, Wx, ba, bx, Lambda, out):
         xs, fs, hs, grps, codes, scales, zs = {}, {}, {}, {}, {}, {}, {}
         tas, ps, a2s, qs, rs = {}, {}, {}, {}, {}
 
+        vt = const.tile([P, P], F32, name="vt")
+        nc.gpsimd.memset(vt[:], 0.0)
         ident = const.tile([P, P], F32, name="ident")
         make_identity(nc, ident[:])
-        vt = const.tile([P, P], F32, name="vt")
-        nc.vector.memset(vt[:], 0.0)
-        one = const.tile([P, 1], F32, name="one")
-        nc.vector.memset(one[:], 1.0)
         quarter = const.tile([P, 1], F32, name="quarter")
         nc.vector.memset(quarter[:], 0.25)
         vt_bf = vt[:].bitcast(BF16)
@@ -85,16 +83,18 @@ def tile_cell_t_kernel(tc, xt, ht_minus_1, Wa, Wx, ba, bx, Lambda, out):
             hs[g] = hpool.tile([P, W4], BF16, tag="h", name="h%d" % g)
             nc.sync.dma_start(out=hs[g][:], in_=h_v[g])
 
-        def load_w(u, eng):
+        def load_w(u):
             t = xpool.tile([P, W4], BF16, tag="x", name="w_sb%d" % u)
             for i, w in enumerate((Wa, Wx)):
-                eng.dma_start(out=t[:, i * 1024:(i + 1) * 1024],
-                              in_=w[256 * u:256 * (u + 1), :].rearrange("(m e) k -> m (e k)", e=2))
+                nc.sync.dma_start(out=t[:, i * 1024:(i + 1) * 1024],
+                                  in_=w[256 * u:256 * (u + 1), :].rearrange("(m e) k -> m (e k)", e=2))
             return t
 
-        load_x(0)
-        w_sb = [load_w(0, nc.scalar)]
-        w_sb.append(load_w(1, nc.sync))
+        xs[0] = xpool.tile([P, W4], BF16, tag="x", name="x0")
+        for half in range(2):
+            cols = slice(half * 1024, (half + 1) * 1024)
+            nc.sync.dma_start(out=xs[0][:, cols], in_=x_v[0][:, cols])
+        w_sb = [load_w(0), load_w(1)]
         load_x(1)
         load_x(2)
         load_h(0)
@@ -120,8 +120,7 @@ def tile_cell_t_kernel(tc, xt, ht_minus_1, Wa, Wx, ba, bx, Lambda, out):
                                         sv[:, col + u:col + 256:2], ident[:])
             return bank
 
-        def regroup_half(src, grp, half):
-            bank = quant_transposes(src, half)
+        def regroup(bank, grp, half):
             nc.vector.tensor_copy(
                 out=grp[:, half * 512:(half + 1) * 512].rearrange("p (c u) -> p c u", u=2),
                 in_=bank[:].rearrange("p (u c) -> p c u", u=2))
@@ -129,47 +128,90 @@ def tile_cell_t_kernel(tc, xt, ht_minus_1, Wa, Wx, ba, bx, Lambda, out):
         def new_grp(name):
             return gpool.tile([P, 1024], F32, tag="grp", name="grp_" + name, align_bytes=64)
 
-        def quantise(grp, cod, sca):
-            nc.vector.quantize_mx(out=cod[:].bitcast(FP8X4), scales=sca[:],
-                                  in_=grp[:].bitcast(BF16))
+        def quantise(grp, cod, sca, lo=0, hi=GB):
+            nc.vector.quantize_mx(out=cod[:, lo:hi].bitcast(FP8X4), scales=sca[:, lo:hi],
+                                  in_=grp[:, 2 * lo:2 * hi].bitcast(BF16))
 
         def prep_x(g, half):
             if half == 0:
                 grps[g] = new_grp("x%d" % g)
-            regroup_half(xs[g], grps[g], half)
+            regroup(quant_transposes(xs[g], half), grps[g], half)
 
         def quant_x(g):
             codes[g] = cpool.tile([P, GB], U32, tag="cod", name="cod%d" % g, align_bytes=64)
             scales[g] = cpool.tile([P, GB], U8, tag="sca", name="sca%d" % g, align_bytes=64)
             quantise(grps[g], codes[g], scales[g])
 
-        cbank = tbank()
-        nc.tensor.transpose(cbank[:, 0:P], vt[:], ident[:])
-        raw = const.tile([P, 12], F32, name="raw")
-        nc.vector.tensor_copy(out=raw[:], in_=cbank[:].bitcast(BF16)[:, 0:12])
-        hb = const.tile([P, 8], F32, name="hb")
-        nc.vector.tensor_scalar_mul(out=hb[:], in0=raw[:, 0:8], scalar1=0.5)
-        lam = raw[:, 8:12]
-        sp_a = const.tile([P, 4], F32, name="sp_a")
-        nc.scalar.activation(out=sp_a[:], in_=lam, func=ACT.Abs)
-        sp_e = const.tile([P, 4], F32, name="sp_e")
-        nc.scalar.activation(out=sp_e[:], in_=sp_a[:], func=ACT.Exp, scale=-1.0)
-        sp_l = const.tile([P, 4], F32, name="sp_l")
-        nc.scalar.activation(out=sp_l[:], in_=sp_e[:], func=ACT.Ln, bias=one[:])
-
-        wcod, wsca, wgrp = [], [], []
+        wcod, wsca = [], []
         for u in range(2):
             wcod.append(const.tile([P, D], U32, name="wcod%d" % u, align_bytes=64))
             wsca.append(const.tile([P, D], U8, name="wsca%d" % u, align_bytes=64))
-        prep_x(0, 0)
-        prep_x(0, 1)
-        wgrp.append(new_grp("w0"))
-        regroup_half(w_sb[0], wgrp[0], 0)
-        regroup_half(w_sb[0], wgrp[0], 1)
-        quant_x(0)
-        quantise(wgrp[0], wcod[0], wsca[0])
-        sp = const.tile([P, 4], F32, name="sp")
+        grps[0] = new_grp("x0")
+        x0_banks = [quant_transposes(xs[0], 0), quant_transposes(xs[0], 1)]
+        cbank = tbank()
+        nc.tensor.transpose(cbank[:, 0:P], vt[:], ident[:])
+        vecs = cbank[:].bitcast(BF16)
+        w0_banks = [quant_transposes(w_sb[0], 0)]
+
+        e_abs = const.tile([P, 4], F32, name="e_abs")
+        nc.scalar.activation(out=e_abs[:], in_=vecs[:, 8:12], func=ACT.Abs)
+        e_neg = const.tile([P, 4], F32, name="e_neg")
+        nc.scalar.activation(out=e_neg[:], in_=e_abs[:], func=ACT.Exp, scale=-1.0)
+
+        regroup(x0_banks[0], grps[0], 0)
+        regroup(x0_banks[1], grps[0], 1)
+        raw = const.tile([P, 12], F32, name="raw")
+        nc.vector.tensor_copy(out=raw[:], in_=vecs[:, 0:12])
+        hb = const.tile([P, 8], F32, name="hb")
+        nc.vector.tensor_scalar_mul(out=hb[:], in0=raw[:, 0:8], scalar1=0.5)
+
+        lam4 = const.tile([P, 4], F32, name="lam4")
+        den = const.tile([P, 4], F32, name="den")
+        inv = const.tile([P, 4], F32, name="inv")
+        z1 = const.tile([P, 4], F32, name="z1")
+        z2 = const.tile([P, 4], F32, name="z2")
+        ser = const.tile([P, 4], F32, name="ser")
+        art = const.tile([P, 4], F32, name="art")
         nc4 = const.tile([P, 4], F32, name="nc4")
+
+        def series_steps():
+            steps = [
+                lambda: nc.vector.tensor_scalar(out=lam4[:], in0=raw[:, 8:12], scalar1=0.0, scalar2=-4.0,
+                                                op0=ALU.max, op1=ALU.mult),
+                lambda: nc.vector.tensor_scalar_add(out=den[:], in0=e_neg[:], scalar1=2.0),
+                lambda: nc.vector.reciprocal(out=inv[:], in_=den[:]),
+                lambda: nc.vector.tensor_tensor(out=z1[:], in0=e_neg[:], in1=inv[:], op=ALU.mult),
+                lambda: nc.vector.tensor_tensor(out=z2[:], in0=z1[:], in1=z1[:], op=ALU.mult),
+                lambda: nc.vector.tensor_scalar_mul(out=ser[:], in0=z2[:], scalar1=1.0 / 19.0),
+            ]
+            for n in range(17, 1, -2):
+                steps.append(lambda n=n: nc.vector.scalar_tensor_tensor(
+                    out=ser[:], in0=ser[:], scalar=1.0 / n, in1=z2[:], op0=ALU.add, op1=ALU.mult))
+            steps.append(lambda: nc.vector.scalar_tensor_tensor(
+                out=art[:], in0=ser[:], scalar=1.0, in1=z1[:], op0=ALU.add, op1=ALU.mult))
+            steps.append(lambda: nc.vector.scalar_tensor_tensor(
+                out=nc4[:], in0=art[:], scalar=-8.0, in1=lam4[:], op0=ALU.mult, op1=ALU.add))
+            return steps
+
+        series = series_steps()
+
+        def run_series(count):
+            for i in range(min(count, len(series))):
+                series.pop(0)()
+
+        wgrp = [new_grp("w0")]
+        regroup(w0_banks[0], wgrp[0], 0)
+        run_series(2)
+        quant_x(0)
+        run_series(1)
+        quantise(wgrp[0], wcod[0], wsca[0], 0, 256)
+        run_series(1)
+        w0_banks.append(quant_transposes(w_sb[0], 1))
+        w1_banks = [quant_transposes(w_sb[1], 0)]
+        regroup(w0_banks[1], wgrp[0], 1)
+        run_series(2)
+        quantise(wgrp[0], wcod[0], wsca[0], 256, 512)
+        run_series(2)
 
         def mx(g, gate, u):
             for e in range(2):
@@ -274,22 +316,17 @@ def tile_cell_t_kernel(tc, xt, ht_minus_1, Wa, Wx, ba, bx, Lambda, out):
             nc.sync.dma_start(out=o_v[g], in_=rs[g][:])
 
         seen_codes = const.tile([P, 1], U32, name="seen_codes")
-        seen_f = const.tile([P, 1], F32, name="seen_f")
 
         def gpsimd_after_quant(g):
             nc.gpsimd.tensor_copy(out=seen_codes[:], in_=codes[g][:, 0:1])
 
-        def gpsimd_after_gmul(g):
-            nc.gpsimd.tensor_copy(out=seen_f[:], in_=ps[g][:, W4 - 1:W4])
-
         mx(0, 0, 0)
         mx(0, 1, 0)
+        w1_banks.append(quant_transposes(w_sb[1], 1))
         wgrp.append(new_grp("w1"))
-        regroup_half(w_sb[1], wgrp[1], 0)
-        regroup_half(w_sb[1], wgrp[1], 1)
-        nc.vector.scalar_tensor_tensor(out=sp[:], in0=lam, scalar=0.0, in1=sp_l[:],
-                                       op0=ALU.max, op1=ALU.add)
-        nc.vector.tensor_scalar_mul(out=nc4[:], in0=sp[:], scalar1=-4.0)
+        regroup(w1_banks[0], wgrp[1], 0)
+        run_series(len(series))
+        regroup(w1_banks[1], wgrp[1], 1)
         quantise(wgrp[1], wcod[1], wsca[1])
         prep_x(1, 0)
         prep_x(1, 1)
@@ -355,10 +392,7 @@ def tile_cell_t_kernel(tc, xt, ht_minus_1, Wa, Wx, ba, bx, Lambda, out):
                         quantised = unquantised.pop(0)
                     if g > 1:
                         gpsimd_after_quant(quantised)
-                if last_chunk and j == 0:
-                    gmul(g - 1, nc.vector, 1)
-                    gpsimd_after_gmul(g - 1)
-                if late_gmul and not (last_chunk and j == 1):
+                if late_gmul and not last_chunk:
                     gmul(late_gmul.pop(0), nc.gpsimd, 1)
                 act_a(g, 0)
                 act_b(g, 0)
@@ -426,7 +460,4 @@ def tile_cell_t_kernel(tc, xt, ht_minus_1, Wa, Wx, ba, bx, Lambda, out):
                         gmul(g, nc.gpsimd, 1)
                     else:
                         late_gmul.append(g)
-                if ci == len(CHUNKS) - 2:
-                    late_gmul.pop()
-                    chunk = [chunk[0], last] + chunk[1:-1]
             pending = pending + chunk

@@ -23,9 +23,9 @@ NT = 4
 LH = 2
 LF = 4
 LEAD = 9
-NOW_GMUL = (3, 3, 3)
+NOW_GMUL = (2, 3, 3)
 MX_POS = 2
-SLOTS = (0, 4, 1)
+SLOTS = (0, 5, 0)
 PREP = {0: (2, 3,), 1: (4, 5,), 2: (6, 7,), 3: (8, 9,), 4: (10, 11,), 5: (12,), 8: (13,), 10: (14, 15,)}
 
 
@@ -60,6 +60,8 @@ def tile_cell_t_kernel(tc, xt, ht_minus_1, Wa, Wx, ba, bx, Lambda, out):
         xs, fs, hs, grps, codes, scales, zs = {}, {}, {}, {}, {}, {}, {}
         tas, ps, a2s, qs, rs = {}, {}, {}, {}, {}
 
+        zeros = const.tile([P, 512], BF16, name="zeros")
+        nc.gpsimd.memset(zeros[:].bitcast(U32), 0)
         vt = const.tile([P, P], F32, name="vt")
         nc.gpsimd.memset(vt[:], 0.0)
         ident = const.tile([P, P], F32, name="ident")
@@ -97,8 +99,6 @@ def tile_cell_t_kernel(tc, xt, ht_minus_1, Wa, Wx, ba, bx, Lambda, out):
         w_sb = [load_w(0), load_w(1)]
         load_x(1)
         load_x(2)
-        load_h(0)
-        load_h(1)
 
         def word_transposes(src, half):
             sv = src[:].bitcast(F32)
@@ -146,8 +146,13 @@ def tile_cell_t_kernel(tc, xt, ht_minus_1, Wa, Wx, ba, bx, Lambda, out):
         for u in range(2):
             wcod.append(const.tile([P, D], U32, name="wcod%d" % u, align_bytes=64))
             wsca.append(const.tile([P, D], U8, name="wsca%d" % u, align_bytes=64))
+        for i in range(6):
+            z = psum.tile([P, 512], F32, tag="Z%d" % (i % 4), name="warm_up%d" % i)
+            nc.tensor.matmul(z[:], lhsT=zeros[:, 0:P], rhs=zeros[:], start=True, stop=True)
         grps[0] = new_grp("x0")
         x0_banks = [quant_transposes(xs[0], 0), quant_transposes(xs[0], 1)]
+        load_x(3)
+        load_h(0)
         cbank = tbank()
         nc.tensor.transpose(cbank[:, 0:P], vt[:], ident[:])
         vecs = cbank[:].bitcast(BF16)
@@ -208,6 +213,8 @@ def tile_cell_t_kernel(tc, xt, ht_minus_1, Wa, Wx, ba, bx, Lambda, out):
         run_series(1)
         w0_banks.append(quant_transposes(w_sb[0], 1))
         w1_banks = [quant_transposes(w_sb[1], 0)]
+        load_x(4)
+        load_h(1)
         regroup(w0_banks[1], wgrp[0], 1)
         run_series(2)
         quantise(wgrp[0], wcod[0], wsca[0], 256, 512)
@@ -301,6 +308,10 @@ def tile_cell_t_kernel(tc, xt, ht_minus_1, Wa, Wx, ba, bx, Lambda, out):
             qs[g] = apool.tile([P, W4], F32, tag="a2", name="q%d" % g)
             nc.scalar.activation(out=qs[g][:], in_=a2s[g][:], func=ACT.Square)
 
+        def act_e_quarter(g, jj):
+            qv = qs[g][:].rearrange("p (k n) -> p k n", k=4)[:, :, jj * P:(jj + 1) * P]
+            nc.scalar.activation(out=qv, in_=qv, func=ACT.Sqrt, scale=-0.25, bias=quarter[:])
+
         def square_apart(g):
             qs[g] = apool.tile([P, W4], F32, tag="a2", name="q%d" % g)
             nc.gpsimd.tensor_tensor(out=qs[g][:], in0=a2s[g][:], in1=a2s[g][:], op=ALU.mult)
@@ -330,7 +341,7 @@ def tile_cell_t_kernel(tc, xt, ht_minus_1, Wa, Wx, ba, bx, Lambda, out):
         quantise(wgrp[1], wcod[1], wsca[1])
         prep_x(1, 0)
         prep_x(1, 1)
-        loaded = {"x": 3, "h": 2, "f": 0}
+        loaded = {"x": 5, "h": 2, "f": 0}
         loaders = {"x": load_x, "h": load_h, "f": load_f}
 
         def load_up_to(kind, g):
@@ -417,9 +428,11 @@ def tile_cell_t_kernel(tc, xt, ht_minus_1, Wa, Wx, ba, bx, Lambda, out):
             last = chunk[-1]
             if last_chunk:
                 for g in chunk[:-1]:
-                    act_e_aside(g)
+                    for jj in range(4):
+                        act_e_quarter(g, jj)
                 square_on_scalar(last)
-                act_e_aside(last)
+                for jj in range(4):
+                    act_e_quarter(last, jj)
                 for jj in range(4):
                     at_h(last, jj)
                 fmul(last, 0)
@@ -431,11 +444,13 @@ def tile_cell_t_kernel(tc, xt, ht_minus_1, Wa, Wx, ba, bx, Lambda, out):
                 for g in chunk[:-1]:
                     for jj in range(4):
                         gmul_quarter(g, jj, nc.gpsimd)
+                for jj in range(2):
+                    gmul_quarter(last, jj, nc.gpsimd)
                 for g in chunk[:-1]:
                     for jj in range(4):
                         finish(g, jj)
                         store_quarter(g, jj)
-                for jj in range(4):
+                for jj in range(2, 4):
                     gmul_quarter(last, jj, nc.vector)
                 for jj in range(4):
                     finish(last, jj)

@@ -15,18 +15,19 @@ ALU = mybir.AluOpType
 
 P = 128
 D = 512
-GB = 512
-NG = 16
-W4 = 4 * GB
+ROWS = 512
+GROUPS = 16
+TILE = 4 * ROWS
+
 CHUNKS = (5, 5, 4, 2)
-NT = 4
-LH = 2
-LF = 4
-LEAD = 9
-NOW_GMUL = (2, 3, 3)
-MX_POS = 2
-SLOTS = (0, 5, 0)
-PREP = {0: (2, 3,), 1: (4, 5,), 2: (6, 7,), 3: (8, 9,), 4: (10, 11,), 5: (12,), 8: (13,), 10: (14, 15,)}
+
+PREPARE = 2
+CODE_TILES = 11
+X_AHEAD = 3
+F_TILES = 4
+WARM_UP = 6
+
+START_NOW = (2, 3, 3)
 
 
 def tile_cell_t_kernel(tc, xt, ht_minus_1, Wa, Wx, ba, bx, Lambda, out):
@@ -34,15 +35,15 @@ def tile_cell_t_kernel(tc, xt, ht_minus_1, Wa, Wx, ba, bx, Lambda, out):
     x_v = xt.rearrange("(g p j) k -> g p (j k)", p=P, j=4)
     h_v = ht_minus_1.rearrange("(g p j) k -> g p (j k)", p=P, j=4)
     o_v = out.rearrange("(g p j) k -> g p (j k)", p=P, j=4)
-    o_v4 = out.rearrange("(g p j) k -> g p j k", p=P, j=4)
+    o_rows = out.rearrange("(g p j) k -> g p j k", p=P, j=4)
 
     with ExitStack() as ctx:
         const = ctx.enter_context(tc.tile_pool(name="const", bufs=1))
         xpool = ctx.enter_context(tc.tile_pool(name="xpool", bufs=5))
-        fpool = ctx.enter_context(tc.tile_pool(name="fpool", bufs=LF))
+        fpool = ctx.enter_context(tc.tile_pool(name="fpool", bufs=F_TILES))
         hpool = ctx.enter_context(tc.tile_pool(name="hpool", bufs=3))
-        gpool = ctx.enter_context(tc.tile_pool(name="gpool", bufs=2))
-        cpool = ctx.enter_context(tc.tile_pool(name="cpool", bufs=LEAD + 2))
+        gpool = ctx.enter_context(tc.tile_pool(name="gpool", bufs=PREPARE))
+        cpool = ctx.enter_context(tc.tile_pool(name="cpool", bufs=CODE_TILES))
         tapool = ctx.enter_context(tc.tile_pool(name="tapool", bufs=1))
         ppool = ctx.enter_context(tc.tile_pool(name="ppool", bufs=max(CHUNKS) + 1))
         apool = ctx.enter_context(tc.tile_pool(name="apool", bufs=max(CHUNKS)))
@@ -50,74 +51,46 @@ def tile_cell_t_kernel(tc, xt, ht_minus_1, Wa, Wx, ba, bx, Lambda, out):
         psum = ctx.enter_context(tc.psum_pool(name="psum", bufs=1))
         ctx.enter_context(tc.manual_schedule())
 
-        tcount = [0]
+        banks_used = [0]
 
-        def tbank():
-            i = tcount[0]
-            tcount[0] = i + 1
-            return psum.tile([P, 512], F32, tag="T%d" % (i % NT), name="T_%d" % i)
+        def transpose_bank():
+            i = banks_used[0]
+            banks_used[0] = i + 1
+            return psum.tile([P, 512], F32, tag="T%d" % (i % 4), name="T_%d" % i)
 
-        xs, fs, hs, grps, codes, scales, zs = {}, {}, {}, {}, {}, {}, {}
+        def gate_bank(i, name):
+            return psum.tile([P, 512], F32, tag="Z%d" % i, name=name)
+
+        xs, fs, hs, grouped, codes, scales, zs = {}, {}, {}, {}, {}, {}, {}
         tas, ps, a2s, qs, rs = {}, {}, {}, {}, {}
 
-        zeros = const.tile([P, 512], BF16, name="zeros")
-        nc.gpsimd.memset(zeros[:].bitcast(U32), 0)
-        vt = const.tile([P, P], F32, name="vt")
-        nc.gpsimd.memset(vt[:], 0.0)
-        ident = const.tile([P, P], F32, name="ident")
-        make_identity(nc, ident[:])
-        quarter = const.tile([P, 1], F32, name="quarter")
-        nc.vector.memset(quarter[:], 0.25)
-        vt_bf = vt[:].bitcast(BF16)
-        for v, vec in enumerate((ba, bx, Lambda)):
-            nc.scalar.dma_start(out=vt_bf[2 * v:2 * v + 2, :],
-                                in_=vec.rearrange("o (u w) -> (o u) w", u=2))
-
         def load_x(g):
-            xs[g] = xpool.tile([P, W4], BF16, tag="x", name="x%d" % g)
+            xs[g] = xpool.tile([P, TILE], BF16, tag="x", name="x%d" % g)
             nc.sync.dma_start(out=xs[g][:], in_=x_v[g])
 
         def load_f(g):
-            fs[g] = fpool.tile([P, W4], BF16, tag="f", name="f%d" % g)
+            fs[g] = fpool.tile([P, TILE], BF16, tag="f", name="f%d" % g)
             nc.sync.dma_start(out=fs[g][:], in_=x_v[g])
 
         def load_h(g):
-            hs[g] = hpool.tile([P, W4], BF16, tag="h", name="h%d" % g)
+            hs[g] = hpool.tile([P, TILE], BF16, tag="h", name="h%d" % g)
             nc.sync.dma_start(out=hs[g][:], in_=h_v[g])
 
         def load_w(u):
-            t = xpool.tile([P, W4], BF16, tag="x", name="w_sb%d" % u)
-            for i, w in enumerate((Wa, Wx)):
-                nc.sync.dma_start(out=t[:, i * 1024:(i + 1) * 1024],
+            t = xpool.tile([P, TILE], BF16, tag="x", name="w_sb%d" % u)
+            for gate, w in enumerate((Wa, Wx)):
+                nc.sync.dma_start(out=t[:, gate * 1024:(gate + 1) * 1024],
                                   in_=w[256 * u:256 * (u + 1), :].rearrange("(m e) k -> m (e k)", e=2))
             return t
 
-        xs[0] = xpool.tile([P, W4], BF16, tag="x", name="x0")
-        for half in range(2):
-            cols = slice(half * 1024, (half + 1) * 1024)
-            nc.sync.dma_start(out=xs[0][:, cols], in_=x_v[0][:, cols])
-        w_sb = [load_w(0), load_w(1)]
-        load_x(1)
-        load_x(2)
-
-        def word_transposes(src, half):
-            sv = src[:].bitcast(F32)
-            bank = tbank()
+        def mx_transposes(src, half):
+            words = src[:].bitcast(F32)
+            bank = transpose_bank()
             for jl in range(2):
+                row = (2 * half + jl) * 256
                 for u in range(2):
-                    col = (2 * half + jl) * 256 + u * 128
-                    nc.tensor.transpose(bank[:, u * 256 + jl * 128:u * 256 + jl * 128 + 128],
-                                        sv[:, col:col + 128], ident[:])
-            return bank
-
-        def quant_transposes(src, half):
-            sv = src[:].bitcast(F32)
-            bank = tbank()
-            for jl in range(2):
-                for u in range(2):
-                    col = (2 * half + jl) * 256
-                    nc.tensor.transpose(bank[:, u * 256 + jl * 128:u * 256 + jl * 128 + 128],
-                                        sv[:, col + u:col + 256:2], ident[:])
+                    col = u * 256 + jl * P
+                    nc.tensor.transpose(bank[:, col:col + P], words[:, row + u:row + 256:2], ident[:])
             return bank
 
         def regroup(bank, grp, half):
@@ -125,106 +98,30 @@ def tile_cell_t_kernel(tc, xt, ht_minus_1, Wa, Wx, ba, bx, Lambda, out):
                 out=grp[:, half * 512:(half + 1) * 512].rearrange("p (c u) -> p c u", u=2),
                 in_=bank[:].rearrange("p (u c) -> p c u", u=2))
 
-        def new_grp(name):
-            return gpool.tile([P, 1024], F32, tag="grp", name="grp_" + name, align_bytes=64)
+        def new_grouped(name):
+            return gpool.tile([P, TILE // 2], F32, tag="grp", name="grp_" + name, align_bytes=64)
 
-        def quantise(grp, cod, sca, lo=0, hi=GB):
+        def quantise(grp, cod, sca, lo=0, hi=ROWS):
             nc.vector.quantize_mx(out=cod[:, lo:hi].bitcast(FP8X4), scales=sca[:, lo:hi],
                                   in_=grp[:, 2 * lo:2 * hi].bitcast(BF16))
 
-        def prep_x(g, half):
+        def prepare_x(g, half):
             if half == 0:
-                grps[g] = new_grp("x%d" % g)
-            regroup(quant_transposes(xs[g], half), grps[g], half)
+                grouped[g] = new_grouped("x%d" % g)
+            regroup(mx_transposes(xs[g], half), grouped[g], half)
 
-        def quant_x(g):
-            codes[g] = cpool.tile([P, GB], U32, tag="cod", name="cod%d" % g, align_bytes=64)
-            scales[g] = cpool.tile([P, GB], U8, tag="sca", name="sca%d" % g, align_bytes=64)
-            quantise(grps[g], codes[g], scales[g])
+        def quantise_x(g):
+            codes[g] = cpool.tile([P, ROWS], U32, tag="cod", name="cod%d" % g, align_bytes=64)
+            scales[g] = cpool.tile([P, ROWS], U8, tag="sca", name="sca%d" % g, align_bytes=64)
+            quantise(grouped[g], codes[g], scales[g])
 
-        wcod, wsca = [], []
-        for u in range(2):
-            wcod.append(const.tile([P, D], U32, name="wcod%d" % u, align_bytes=64))
-            wsca.append(const.tile([P, D], U8, name="wsca%d" % u, align_bytes=64))
-        for i in range(6):
-            z = psum.tile([P, 512], F32, tag="Z%d" % (i % 4), name="warm_up%d" % i)
-            nc.tensor.matmul(z[:], lhsT=zeros[:, 0:P], rhs=zeros[:], start=True, stop=True)
-        grps[0] = new_grp("x0")
-        x0_banks = [quant_transposes(xs[0], 0), quant_transposes(xs[0], 1)]
-        load_x(3)
-        load_h(0)
-        cbank = tbank()
-        nc.tensor.transpose(cbank[:, 0:P], vt[:], ident[:])
-        vecs = cbank[:].bitcast(BF16)
-        w0_banks = [quant_transposes(w_sb[0], 0)]
+        def gpsimd_waits_for_codes(g):
+            nc.gpsimd.tensor_copy(out=seen[:], in_=codes[g][:, 0:1])
 
-        e_abs = const.tile([P, 4], F32, name="e_abs")
-        nc.scalar.activation(out=e_abs[:], in_=vecs[:, 8:12], func=ACT.Abs)
-        e_neg = const.tile([P, 4], F32, name="e_neg")
-        nc.scalar.activation(out=e_neg[:], in_=e_abs[:], func=ACT.Exp, scale=-1.0)
-
-        regroup(x0_banks[0], grps[0], 0)
-        regroup(x0_banks[1], grps[0], 1)
-        raw = const.tile([P, 12], F32, name="raw")
-        nc.vector.tensor_copy(out=raw[:], in_=vecs[:, 0:12])
-        hb = const.tile([P, 8], F32, name="hb")
-        nc.vector.tensor_scalar_mul(out=hb[:], in0=raw[:, 0:8], scalar1=0.5)
-
-        lam4 = const.tile([P, 4], F32, name="lam4")
-        den = const.tile([P, 4], F32, name="den")
-        inv = const.tile([P, 4], F32, name="inv")
-        z1 = const.tile([P, 4], F32, name="z1")
-        z2 = const.tile([P, 4], F32, name="z2")
-        ser = const.tile([P, 4], F32, name="ser")
-        art = const.tile([P, 4], F32, name="art")
-        nc4 = const.tile([P, 4], F32, name="nc4")
-
-        def series_steps():
-            steps = [
-                lambda: nc.vector.tensor_scalar(out=lam4[:], in0=raw[:, 8:12], scalar1=0.0, scalar2=-4.0,
-                                                op0=ALU.max, op1=ALU.mult),
-                lambda: nc.vector.tensor_scalar_add(out=den[:], in0=e_neg[:], scalar1=2.0),
-                lambda: nc.vector.reciprocal(out=inv[:], in_=den[:]),
-                lambda: nc.vector.tensor_tensor(out=z1[:], in0=e_neg[:], in1=inv[:], op=ALU.mult),
-                lambda: nc.vector.tensor_tensor(out=z2[:], in0=z1[:], in1=z1[:], op=ALU.mult),
-                lambda: nc.vector.tensor_scalar_mul(out=ser[:], in0=z2[:], scalar1=1.0 / 19.0),
-            ]
-            for n in range(17, 1, -2):
-                steps.append(lambda n=n: nc.vector.scalar_tensor_tensor(
-                    out=ser[:], in0=ser[:], scalar=1.0 / n, in1=z2[:], op0=ALU.add, op1=ALU.mult))
-            steps.append(lambda: nc.vector.scalar_tensor_tensor(
-                out=art[:], in0=ser[:], scalar=1.0, in1=z1[:], op0=ALU.add, op1=ALU.mult))
-            steps.append(lambda: nc.vector.scalar_tensor_tensor(
-                out=nc4[:], in0=art[:], scalar=-8.0, in1=lam4[:], op0=ALU.mult, op1=ALU.add))
-            return steps
-
-        series = series_steps()
-
-        def run_series(count):
-            for i in range(min(count, len(series))):
-                series.pop(0)()
-
-        wgrp = [new_grp("w0")]
-        regroup(w0_banks[0], wgrp[0], 0)
-        run_series(2)
-        quant_x(0)
-        run_series(1)
-        quantise(wgrp[0], wcod[0], wsca[0], 0, 256)
-        run_series(1)
-        w0_banks.append(quant_transposes(w_sb[0], 1))
-        w1_banks = [quant_transposes(w_sb[1], 0)]
-        load_x(4)
-        load_h(1)
-        regroup(w0_banks[1], wgrp[0], 1)
-        run_series(2)
-        quantise(wgrp[0], wcod[0], wsca[0], 256, 512)
-        run_series(2)
-
-        def mx(g, gate, u):
+        def gate_passes(g, gate, u):
             for e in range(2):
                 col = (2 * gate + e) * P
-                z = psum.tile([P, 512], F32, tag="Z%d" % (2 * gate + e),
-                              name="z%d_%d_%d" % (gate, g, 2 * u + e))
+                z = gate_bank(2 * gate + e, "z%d_%d_%d" % (gate, g, 2 * u + e))
                 nc.tensor.matmul_mx(
                     out=z[:],
                     lhsT=wcod[u][:, col:col + P].bitcast(FP8X4),
@@ -234,245 +131,327 @@ def tile_cell_t_kernel(tc, xt, ht_minus_1, Wa, Wx, ba, bx, Lambda, out):
                     start=True, stop=True)
                 zs[(g, gate, 2 * u + e)] = z
 
-        def act_a(g, u):
+        def tanh_a(g, u):
             if u == 0:
-                tas[g] = tapool.tile([P, W4], F32, tag="ta", name="ta%d" % g)
-            for blk in (2 * u, 2 * u + 1):
-                nc.scalar.activation(out=tas[g][:, blk * GB:(blk + 1) * GB], in_=zs[(g, 0, blk)][:],
-                                     func=ACT.Tanh, scale=0.5, bias=hb[:, blk:blk + 1])
+                tas[g] = tapool.tile([P, TILE], F32, tag="ta", name="ta%d" % g)
+            for b in (2 * u, 2 * u + 1):
+                nc.scalar.activation(out=tas[g][:, b * ROWS:(b + 1) * ROWS], in_=zs[(g, 0, b)][:],
+                                     func=ACT.Tanh, scale=0.5, bias=half_bias[:, b:b + 1])
 
-        def act_b(g, u):
+        def tanh_x(g, u):
             if u == 0:
-                ps[g] = ppool.tile([P, W4], F32, tag="p", name="p%d" % g)
-            for blk in (2 * u, 2 * u + 1):
-                nc.scalar.activation(out=ps[g][:, blk * GB:(blk + 1) * GB], in_=zs[(g, 1, blk)][:],
-                                     func=ACT.Tanh, scale=0.5, bias=hb[:, 4 + blk:5 + blk])
+                ps[g] = ppool.tile([P, TILE], F32, tag="p", name="p%d" % g)
+            for b in (2 * u, 2 * u + 1):
+                nc.scalar.activation(out=ps[g][:, b * ROWS:(b + 1) * ROWS], in_=zs[(g, 1, b)][:],
+                                     func=ACT.Tanh, scale=0.5, bias=half_bias[:, 4 + b:5 + b])
 
-        def act_c(g, u):
+        def exp_a(g, u):
             if u == 0:
-                a2s[g] = apool.tile([P, W4], F32, tag="a2", name="a2_%d" % g)
-            for blk in (2 * u, 2 * u + 1):
-                nc.scalar.activation(out=a2s[g][:, blk * GB:(blk + 1) * GB],
-                                     in_=tas[g][:, blk * GB:(blk + 1) * GB],
-                                     func=ACT.Exp, scale=nc4[:, blk:blk + 1], bias=nc4[:, blk:blk + 1])
+                a2s[g] = apool.tile([P, TILE], F32, tag="a2", name="a2_%d" % g)
+            for b in (2 * u, 2 * u + 1):
+                nc.scalar.activation(out=a2s[g][:, b * ROWS:(b + 1) * ROWS],
+                                     in_=tas[g][:, b * ROWS:(b + 1) * ROWS],
+                                     func=ACT.Exp, scale=nc4[:, b:b + 1], bias=nc4[:, b:b + 1])
 
-        def back_transposes(src, jj):
-            bank = tbank()
-            for blk in range(4):
-                nc.tensor.transpose(bank[:, blk * P:(blk + 1) * P],
-                                    src[:, blk * GB + jj * P:blk * GB + (jj + 1) * P], ident[:])
+        def sqrt(ap):
+            nc.scalar.activation(out=ap, in_=ap, func=ACT.Sqrt, scale=-0.25, bias=quarter[:])
+
+        def rows_of(t, j):
+            return t[:].rearrange("p (b n) -> p b n", b=4)[:, :, j * P:(j + 1) * P]
+
+        def back_transposes(src, j):
+            bank = transpose_bank()
+            for b in range(4):
+                nc.tensor.transpose(bank[:, b * P:(b + 1) * P],
+                                    src[:, b * ROWS + j * P:b * ROWS + (j + 1) * P], ident[:])
             return bank[:].rearrange("p (u e m) -> p u m e", u=2, e=2)
 
-        def nat(t, jj):
-            return t[:, jj * D:(jj + 1) * D].rearrange("p (u m e) -> p u m e", u=2, e=2)
+        def row(t, j):
+            return t[:, j * D:(j + 1) * D].rearrange("p (u m e) -> p u m e", u=2, e=2)
 
-        def at_h(g, jj):
-            if jj == 0:
-                rs[g] = rpool.tile([P, W4], F32, tag="r", name="r%d" % g)
-            bv = back_transposes(a2s[g], jj)
-            nc.vector.tensor_tensor(out=nat(rs[g], jj), in0=bv, in1=nat(hs[g], jj), op=ALU.mult)
+        def times_h(g, j):
+            if j == 0:
+                rs[g] = rpool.tile([P, TILE], F32, tag="r", name="r%d" % g)
+            nc.vector.tensor_tensor(out=row(rs[g], j), in0=back_transposes(a2s[g], j), in1=row(hs[g], j),
+                                    op=ALU.mult)
 
-        def square(g):
-            nc.gpsimd.tensor_tensor(out=a2s[g][:], in0=a2s[g][:], in1=a2s[g][:], op=ALU.mult)
+        def finish(g, j):
+            nc.vector.tensor_tensor(out=row(rs[g], j), in0=back_transposes(ps[g], j), in1=row(rs[g], j),
+                                    op=ALU.add)
 
-        def act_e(g):
-            nc.scalar.activation(out=a2s[g][:], in_=a2s[g][:], func=ACT.Sqrt, scale=-0.25,
-                                 bias=quarter[:])
-
-        def fmul(g, half):
-            pv = ps[g][:].rearrange("p (k n) -> p k n", k=4)
-            bv = word_transposes(fs[g], half)[:].bitcast(BF16)
+        def times_x(g, half):
+            words = fs[g][:].bitcast(F32)
+            bank = transpose_bank()
+            for jl in range(2):
+                for u in range(2):
+                    col = (2 * half + jl) * 256 + u * P
+                    nc.tensor.transpose(bank[:, u * 256 + jl * P:u * 256 + (jl + 1) * P],
+                                        words[:, col:col + P], ident[:])
+            x_bf = bank[:].bitcast(BF16)
+            blocks = ps[g][:].rearrange("p (b n) -> p b n", b=4)
             for u in range(2):
-                io = pv[:, 2 * u:2 * u + 2, half * 256:(half + 1) * 256]
+                io = blocks[:, 2 * u:2 * u + 2, half * 256:(half + 1) * 256]
                 nc.vector.scalar_tensor_tensor(
                     out=io, in0=io, scalar=1.0,
-                    in1=bv[:, u * 512:(u + 1) * 512].rearrange("p (c e) -> p e c", e=2),
+                    in1=x_bf[:, u * 512:(u + 1) * 512].rearrange("p (c e) -> p e c", e=2),
                     op0=ALU.add, op1=ALU.mult)
 
-        def gmul(g, eng, parts):
-            w = W4 // parts
-            for i in range(parts):
-                eng.tensor_tensor(out=ps[g][:, i * w:(i + 1) * w], in0=ps[g][:, i * w:(i + 1) * w],
-                                  in1=a2s[g][:, i * w:(i + 1) * w], op=ALU.mult)
+        def square_in_place(g):
+            nc.gpsimd.tensor_tensor(out=a2s[g][:], in0=a2s[g][:], in1=a2s[g][:], op=ALU.mult)
 
-        def gmul_quarter(g, jj, eng):
-            pv = ps[g][:].rearrange("p (k n) -> p k n", k=4)[:, :, jj * P:(jj + 1) * P]
-            sv = qs.get(g, a2s[g])[:].rearrange("p (k n) -> p k n", k=4)[:, :, jj * P:(jj + 1) * P]
-            eng.tensor_tensor(out=pv, in0=pv, in1=sv, op=ALU.mult)
+        def new_squares(g):
+            qs[g] = apool.tile([P, TILE], F32, tag="a2", name="q%d" % g)
+            return qs[g]
 
-        def act_e_aside(g):
-            nc.scalar.activation(out=qs[g][:], in_=qs[g][:], func=ACT.Sqrt, scale=-0.25,
-                                 bias=quarter[:])
+        def product(g):
+            nc.gpsimd.tensor_tensor(out=ps[g][:], in0=ps[g][:], in1=a2s[g][:], op=ALU.mult)
 
-        def square_on_scalar(g):
-            qs[g] = apool.tile([P, W4], F32, tag="a2", name="q%d" % g)
-            nc.scalar.activation(out=qs[g][:], in_=a2s[g][:], func=ACT.Square)
-
-        def act_e_quarter(g, jj):
-            qv = qs[g][:].rearrange("p (k n) -> p k n", k=4)[:, :, jj * P:(jj + 1) * P]
-            nc.scalar.activation(out=qv, in_=qv, func=ACT.Sqrt, scale=-0.25, bias=quarter[:])
-
-        def square_apart(g):
-            qs[g] = apool.tile([P, W4], F32, tag="a2", name="q%d" % g)
-            nc.gpsimd.tensor_tensor(out=qs[g][:], in0=a2s[g][:], in1=a2s[g][:], op=ALU.mult)
-
-        def store_quarter(g, jj):
-            nc.sync.dma_start(out=o_v4[g][:, jj, :], in_=rs[g][:, jj * D:(jj + 1) * D])
-
-        def finish(g, jj):
-            bv = back_transposes(ps[g], jj)
-            nc.vector.tensor_tensor(out=nat(rs[g], jj), in0=bv, in1=nat(rs[g], jj), op=ALU.add)
+        def product_rows(g, j, engine):
+            io = rows_of(ps[g], j)
+            engine.tensor_tensor(out=io, in0=io, in1=rows_of(qs[g], j), op=ALU.mult)
 
         def store(g):
             nc.sync.dma_start(out=o_v[g], in_=rs[g][:])
 
-        seen_codes = const.tile([P, 1], U32, name="seen_codes")
+        def store_rows(g, j):
+            nc.sync.dma_start(out=o_rows[g][:, j, :], in_=rs[g][:, j * D:(j + 1) * D])
 
-        def gpsimd_after_quant(g):
-            nc.gpsimd.tensor_copy(out=seen_codes[:], in_=codes[g][:, 0:1])
+        zeros = const.tile([P, 512], BF16, name="zeros")
+        nc.gpsimd.memset(zeros[:].bitcast(U32), 0)
+        vectors = const.tile([P, P], F32, name="vt")
+        nc.gpsimd.memset(vectors[:], 0.0)
+        ident = const.tile([P, P], F32, name="ident")
+        make_identity(nc, ident[:])
+        quarter = const.tile([P, 1], F32, name="quarter")
+        nc.vector.memset(quarter[:], 0.25)
+        for v, vec in enumerate((ba, bx, Lambda)):
+            nc.scalar.dma_start(out=vectors[:].bitcast(BF16)[2 * v:2 * v + 2, :],
+                                in_=vec.rearrange("o (u w) -> (o u) w", u=2))
 
-        mx(0, 0, 0)
-        mx(0, 1, 0)
-        w1_banks.append(quant_transposes(w_sb[1], 1))
-        wgrp.append(new_grp("w1"))
-        regroup(w1_banks[0], wgrp[1], 0)
+        xs[0] = xpool.tile([P, TILE], BF16, tag="x", name="x0")
+        for half in range(2):
+            cols = slice(half * 1024, (half + 1) * 1024)
+            nc.sync.dma_start(out=xs[0][:, cols], in_=x_v[0][:, cols])
+        w_sb = [load_w(0), load_w(1)]
+        load_x(1)
+        load_x(2)
+
+        seen = const.tile([P, 1], U32, name="seen_codes")
+        wcod, wsca = [], []
+        for u in range(2):
+            wcod.append(const.tile([P, D], U32, name="wcod%d" % u, align_bytes=64))
+            wsca.append(const.tile([P, D], U8, name="wsca%d" % u, align_bytes=64))
+
+        for i in range(WARM_UP):
+            z = gate_bank(i % 4, "warm_up%d" % i)
+            nc.tensor.matmul(z[:], lhsT=zeros[:, 0:P], rhs=zeros[:], start=True, stop=True)
+        grouped[0] = new_grouped("x0")
+        x0_banks = [mx_transposes(xs[0], 0), mx_transposes(xs[0], 1)]
+        load_x(3)
+        load_h(0)
+        vector_bank = transpose_bank()
+        nc.tensor.transpose(vector_bank[:, 0:P], vectors[:], ident[:])
+        vec_bf = vector_bank[:].bitcast(BF16)
+        w0_banks = [mx_transposes(w_sb[0], 0)]
+
+        e_abs = const.tile([P, 4], F32, name="e_abs")
+        nc.scalar.activation(out=e_abs[:], in_=vec_bf[:, 8:12], func=ACT.Abs)
+        e_neg = const.tile([P, 4], F32, name="e_neg")
+        nc.scalar.activation(out=e_neg[:], in_=e_abs[:], func=ACT.Exp, scale=-1.0)
+
+        regroup(x0_banks[0], grouped[0], 0)
+        regroup(x0_banks[1], grouped[0], 1)
+        raw = const.tile([P, 12], F32, name="raw")
+        nc.vector.tensor_copy(out=raw[:], in_=vec_bf[:, 0:12])
+        half_bias = const.tile([P, 8], F32, name="hb")
+        nc.vector.tensor_scalar_mul(out=half_bias[:], in0=raw[:, 0:8], scalar1=0.5)
+
+        lam4, den, inv, z1, z2, z4, odd, even, art, nc4 = [
+            const.tile([P, 4], F32, name=name)
+            for name in ("lam4", "den", "inv", "z1", "z2", "z4", "odd", "even", "art", "nc4")]
+
+        def horner(acc, n):
+            return lambda: nc.vector.scalar_tensor_tensor(
+                out=acc[:], in0=acc[:], scalar=1.0 / n, in1=z4[:], op0=ALU.add, op1=ALU.mult)
+
+        series = [
+            lambda: nc.vector.tensor_scalar(out=lam4[:], in0=raw[:, 8:12], scalar1=0.0, scalar2=-4.0,
+                                            op0=ALU.max, op1=ALU.mult),
+            lambda: nc.vector.tensor_scalar_add(out=den[:], in0=e_neg[:], scalar1=2.0),
+            lambda: nc.vector.reciprocal(out=inv[:], in_=den[:]),
+            lambda: nc.vector.tensor_tensor(out=z1[:], in0=e_neg[:], in1=inv[:], op=ALU.mult),
+            lambda: nc.vector.tensor_tensor(out=z2[:], in0=z1[:], in1=z1[:], op=ALU.mult),
+            lambda: nc.vector.tensor_tensor(out=z4[:], in0=z2[:], in1=z2[:], op=ALU.mult),
+            lambda: nc.vector.tensor_scalar_mul(out=odd[:], in0=z4[:], scalar1=1.0 / 19.0),
+            lambda: nc.vector.tensor_scalar_mul(out=even[:], in0=z4[:], scalar1=1.0 / 17.0),
+            horner(odd, 15), horner(even, 13), horner(odd, 11), horner(even, 9), horner(odd, 7),
+            lambda: nc.vector.scalar_tensor_tensor(out=even[:], in0=even[:], scalar=1.0 / 5.0, in1=z2[:],
+                                                   op0=ALU.add, op1=ALU.mult),
+            lambda: nc.vector.scalar_tensor_tensor(out=odd[:], in0=odd[:], scalar=1.0 / 3.0, in1=even[:],
+                                                   op0=ALU.add, op1=ALU.add),
+            lambda: nc.vector.tensor_tensor(out=odd[:], in0=odd[:], in1=z2[:], op=ALU.mult),
+            lambda: nc.vector.scalar_tensor_tensor(out=art[:], in0=odd[:], scalar=1.0, in1=z1[:],
+                                                   op0=ALU.add, op1=ALU.mult),
+            lambda: nc.vector.scalar_tensor_tensor(out=nc4[:], in0=art[:], scalar=-8.0, in1=lam4[:],
+                                                   op0=ALU.mult, op1=ALU.add),
+        ]
+
+        def run_series(count):
+            for i in range(count):
+                series.pop(0)()
+
+        w_grouped = [new_grouped("w0")]
+        regroup(w0_banks[0], w_grouped[0], 0)
+        run_series(2)
+        quantise_x(0)
+        run_series(1)
+        quantise(w_grouped[0], wcod[0], wsca[0], 0, 256)
+        run_series(1)
+        w0_banks.append(mx_transposes(w_sb[0], 1))
+        w1_banks = [mx_transposes(w_sb[1], 0)]
+        load_x(4)
+        load_h(1)
+        regroup(w0_banks[1], w_grouped[0], 1)
+        run_series(1)
+        quantise(w_grouped[0], wcod[0], wsca[0], 256, 512)
+        run_series(1)
+        gate_passes(0, 0, 0)
+        gate_passes(0, 1, 0)
+        w1_banks.append(mx_transposes(w_sb[1], 1))
+        w_grouped.append(new_grouped("w1"))
+        regroup(w1_banks[0], w_grouped[1], 0)
         run_series(len(series))
-        regroup(w1_banks[1], wgrp[1], 1)
-        quantise(wgrp[1], wcod[1], wsca[1])
-        prep_x(1, 0)
-        prep_x(1, 1)
-        loaded = {"x": 5, "h": 2, "f": 0}
+        regroup(w1_banks[1], w_grouped[1], 1)
+        quantise(w_grouped[1], wcod[1], wsca[1])
+        prepare_x(1, 0)
+        prepare_x(1, 1)
+
         loaders = {"x": load_x, "h": load_h, "f": load_f}
+        loaded = {"x": 5, "h": 2, "f": 0}
 
         def load_up_to(kind, g):
-            while loaded[kind] < NG and loaded[kind] <= g:
+            while loaded[kind] < GROUPS and loaded[kind] <= g:
                 loaders[kind](loaded[kind])
                 loaded[kind] += 1
 
-        pending = []
-        unquantised = [1]
         prepared = 1
-        late_gmul = []
-        g0 = 0
+        to_quantise = [1]
+        to_multiply = []
+        to_finish = []
+        first = 0
         for ci, n in enumerate(CHUNKS):
-            chunk = list(range(g0, g0 + n))
-            g0 += n
-            last_chunk = ci == len(CHUNKS) - 1
-            per_step = -(-len(pending) // n)
-            for j, g in enumerate(chunk):
-                now, pending = pending[:per_step], pending[per_step:]
-                if last_chunk and j == n - 1:
-                    now, pending = now[:1], now[1:]
-                banks = []
-                if j > 0:
-                    banks.extend([("R", g - 1, jj) for jj in range(4)])
-                for pg in now:
-                    banks.extend([("O", pg, jj) for jj in range(4)])
-                if last_chunk and j < n - 1:
-                    banks.extend([("F", g, 0), ("F", g, 1)])
-                for k in PREP.get(g, ()):
-                    banks.extend([("K", k, 0), ("K", k, 1)])
-                    prepared = k
-                load_up_to("x", prepared + 3)
-                load_up_to("h", g + LH - 1)
-                load_up_to("f", g if last_chunk else g - 1 if j > 0 else -1)
-                pos = [0]
+            chunk = list(range(first, first + n))
+            first += n
+            is_last = ci == len(CHUNKS) - 1
+            finish_per_step = -(-len(to_finish) // n)
+            for i, g in enumerate(chunk):
+                ends_kernel = is_last and i == n - 1
+                count = 1 if ends_kernel else finish_per_step
+                finishing, to_finish = to_finish[:count], to_finish[count:]
+                work = []
+                if i > 0:
+                    work.extend([(times_h, g - 1, j) for j in range(4)])
+                for done in finishing:
+                    work.extend([(finish, done, j) for j in range(4)])
+                if is_last and i < n - 1:
+                    work.extend([(times_x, g, 0), (times_x, g, 1)])
+                if ci == 0 or i == 0:
+                    for k in range(prepared + 1, min(prepared + 1 + PREPARE, GROUPS)):
+                        work.extend([(prepare_x, k, 0), (prepare_x, k, 1)])
+                        prepared = k
+                load_up_to("x", prepared + X_AHEAD)
+                load_up_to("h", g + 1)
+                load_up_to("f", g if is_last else g - 1 if i > 0 else -1)
+                new_codes = []
 
-                def emit(count):
-                    for kind, gg, part in banks[pos[0]:pos[0] + count]:
-                        if kind == "R":
-                            if part == 0 and last_chunk:
-                                square_apart(gg)
-                                gmul(late_gmul.pop(0), nc.gpsimd, 1)
-                            at_h(gg, part)
-                            if part == 3 and not last_chunk:
-                                square(gg)
-                        elif kind == "K":
-                            prep_x(gg, part)
-                        elif kind == "F":
-                            fmul(gg, part)
-                        else:
-                            finish(gg, part)
-                        if kind == "K" and part == 1:
-                            unquantised.append(gg)
-                    pos[0] += count
+                def run_work(count):
+                    for what, group, part in work[:count]:
+                        if is_last and what is times_h and part == 0:
+                            squares = new_squares(group)
+                            nc.gpsimd.tensor_tensor(out=squares[:], in0=a2s[group][:], in1=a2s[group][:],
+                                                    op=ALU.mult)
+                            product(to_multiply.pop(0))
+                        what(group, part)
+                        if what is times_h and part == 3 and not is_last:
+                            square_in_place(group)
+                        if what is prepare_x and part == 1:
+                            new_codes.append(group)
+                    work[:count] = []
 
-                if unquantised:
-                    while unquantised:
-                        quant_x(unquantised[0])
-                        quantised = unquantised.pop(0)
-                    if g > 1:
-                        gpsimd_after_quant(quantised)
-                if late_gmul and not last_chunk:
-                    gmul(late_gmul.pop(0), nc.gpsimd, 1)
-                act_a(g, 0)
-                act_b(g, 0)
-                if j == 0:
-                    emit(2)
-                mx(g, 0, 1)
-                emit(SLOTS[0])
-                mx(g, 1, 1)
-                act_c(g, 0)
-                act_a(g, 1)
-                act_b(g, 1)
-                emit(SLOTS[1])
-                if j < n - 1:
-                    mx(g + 1, 0, 0)
-                emit(SLOTS[2])
-                if j < n - 1:
-                    mx(g + 1, 1, 0)
-                act_c(g, 1)
-                emit(len(banks))
-                for pg in now:
-                    store(pg)
+                for k in to_quantise:
+                    quantise_x(k)
+                if to_quantise and g > 1:
+                    gpsimd_waits_for_codes(to_quantise[-1])
+                if to_multiply and not is_last:
+                    product(to_multiply.pop(0))
+                tanh_a(g, 0)
+                tanh_x(g, 0)
+                if ci == 0 or i == 0:
+                    run_work(2)
+                gate_passes(g, 0, 1)
+                gate_passes(g, 1, 1)
+                exp_a(g, 0)
+                tanh_a(g, 1)
+                tanh_x(g, 1)
+                run_work(4 if ci == 0 else 5)
+                if i < n - 1:
+                    gate_passes(g + 1, 0, 0)
+                    gate_passes(g + 1, 1, 0)
+                exp_a(g, 1)
+                run_work(len(work))
+                to_quantise = new_codes
+                for done in finishing:
+                    store(done)
+
             last = chunk[-1]
-            if last_chunk:
-                for g in chunk[:-1]:
-                    for jj in range(4):
-                        act_e_quarter(g, jj)
-                square_on_scalar(last)
-                for jj in range(4):
-                    act_e_quarter(last, jj)
-                for jj in range(4):
-                    at_h(last, jj)
-                fmul(last, 0)
-                fmul(last, 1)
-                for pg in pending:
-                    for jj in range(4):
-                        finish(pg, jj)
-                    store(pg)
-                for g in chunk[:-1]:
-                    for jj in range(4):
-                        gmul_quarter(g, jj, nc.gpsimd)
-                for jj in range(2):
-                    gmul_quarter(last, jj, nc.gpsimd)
-                for g in chunk[:-1]:
-                    for jj in range(4):
-                        finish(g, jj)
-                        store_quarter(g, jj)
-                for jj in range(2, 4):
-                    gmul_quarter(last, jj, nc.vector)
-                for jj in range(4):
-                    finish(last, jj)
-                    store_quarter(last, jj)
-            else:
-                while unquantised:
-                    quant_x(unquantised[0])
-                    quantised = unquantised.pop(0)
-                    gpsimd_after_quant(quantised)
-                for jj in range(4):
-                    at_h(last, jj)
-                square(last)
+            if not is_last:
+                for k in to_quantise:
+                    quantise_x(k)
+                    gpsimd_waits_for_codes(k)
+                to_quantise = []
+                for j in range(4):
+                    times_h(last, j)
+                square_in_place(last)
                 for i, g in enumerate(chunk):
-                    load_up_to("f", min(g + LF - 1, last))
-                    if i == MX_POS:
-                        mx(last + 1, 0, 0)
-                        mx(last + 1, 1, 0)
-                    act_e(g)
-                    fmul(g, 0)
-                    fmul(g, 1)
-                    if i < NOW_GMUL[ci]:
-                        gmul(g, nc.gpsimd, 1)
+                    load_up_to("f", min(g + F_TILES - 1, last))
+                    if i == 2:
+                        gate_passes(last + 1, 0, 0)
+                        gate_passes(last + 1, 1, 0)
+                    sqrt(a2s[g][:])
+                    times_x(g, 0)
+                    times_x(g, 1)
+                    if i < START_NOW[ci]:
+                        product(g)
                     else:
-                        late_gmul.append(g)
-            pending = pending + chunk
+                        to_multiply.append(g)
+                to_finish = to_finish + chunk
+
+        early, last = chunk[:-1], chunk[-1]
+        for g in early:
+            for j in range(4):
+                sqrt(rows_of(qs[g], j))
+        nc.scalar.activation(out=new_squares(last)[:], in_=a2s[last][:], func=ACT.Square)
+        for j in range(4):
+            sqrt(rows_of(qs[last], j))
+        for j in range(4):
+            times_h(last, j)
+        times_x(last, 0)
+        times_x(last, 1)
+        for g in to_finish:
+            for j in range(4):
+                finish(g, j)
+            store(g)
+        for g in early:
+            for j in range(4):
+                product_rows(g, j, nc.gpsimd)
+        for j in range(2):
+            product_rows(last, j, nc.gpsimd)
+        for g in early:
+            for j in range(4):
+                finish(g, j)
+                store_rows(g, j)
+        for j in range(2, 4):
+            product_rows(last, j, nc.vector)
+        for j in range(4):
+            finish(last, j)
+            store_rows(last, j)

@@ -25,9 +25,9 @@ PREPARE = 2
 CODE_TILES = 11
 X_AHEAD = 3
 F_TILES = 4
-WARM_UP = 6
+WARM_UP = 4
 
-START_NOW = (2, 3, 3)
+START_NOW = (2, 3, 2)
 
 
 def tile_cell_t_kernel(tc, xt, ht_minus_1, Wa, Wx, ba, bx, Lambda, out):
@@ -93,10 +93,9 @@ def tile_cell_t_kernel(tc, xt, ht_minus_1, Wa, Wx, ba, bx, Lambda, out):
                     nc.tensor.transpose(bank[:, col:col + P], words[:, row + u:row + 256:2], ident[:])
             return bank
 
-        def regroup(bank, grp, half):
-            nc.vector.tensor_copy(
-                out=grp[:, half * 512:(half + 1) * 512].rearrange("p (c u) -> p c u", u=2),
-                in_=bank[:].rearrange("p (u c) -> p c u", u=2))
+        def regroup(bank, grp, half, copy=nc.vector.tensor_copy):
+            copy(out=grp[:, half * 512:(half + 1) * 512].rearrange("p (c u) -> p c u", u=2),
+                 in_=bank[:].rearrange("p (u c) -> p c u", u=2))
 
         def new_grouped(name):
             return gpool.tile([P, TILE // 2], F32, tag="grp", name="grp_" + name, align_bytes=64)
@@ -261,6 +260,7 @@ def tile_cell_t_kernel(tc, xt, ht_minus_1, Wa, Wx, ba, bx, Lambda, out):
 
         regroup(x0_banks[0], grouped[0], 0)
         regroup(x0_banks[1], grouped[0], 1)
+        quantise_x(0)
         raw = const.tile([P, 12], F32, name="raw")
         nc.vector.tensor_copy(out=raw[:], in_=vec_bf[:, 0:12])
         half_bias = const.tile([P, 8], F32, name="hb")
@@ -301,27 +301,26 @@ def tile_cell_t_kernel(tc, xt, ht_minus_1, Wa, Wx, ba, bx, Lambda, out):
                 series.pop(0)()
 
         w_grouped = [new_grouped("w0")]
-        regroup(w0_banks[0], w_grouped[0], 0)
-        run_series(2)
-        quantise_x(0)
-        run_series(1)
+        regroup(w0_banks[0], w_grouped[0], 0, nc.scalar.copy)
+        run_series(3)
         quantise(w_grouped[0], wcod[0], wsca[0], 0, 256)
         run_series(1)
         w0_banks.append(mx_transposes(w_sb[0], 1))
         w1_banks = [mx_transposes(w_sb[1], 0)]
         load_x(4)
         load_h(1)
-        regroup(w0_banks[1], w_grouped[0], 1)
+        regroup(w0_banks[1], w_grouped[0], 1, nc.scalar.copy)
         run_series(1)
         quantise(w_grouped[0], wcod[0], wsca[0], 256, 512)
         run_series(1)
+        w_grouped.append(new_grouped("w1"))
+        regroup(w1_banks[0], w_grouped[1], 0, nc.scalar.copy)
         gate_passes(0, 0, 0)
         gate_passes(0, 1, 0)
         w1_banks.append(mx_transposes(w_sb[1], 1))
-        w_grouped.append(new_grouped("w1"))
-        regroup(w1_banks[0], w_grouped[1], 0)
-        run_series(len(series))
+        run_series(9)
         regroup(w1_banks[1], w_grouped[1], 1)
+        run_series(len(series))
         quantise(w_grouped[1], wcod[1], wsca[1])
         prepare_x(1, 0)
         prepare_x(1, 1)
@@ -343,10 +342,8 @@ def tile_cell_t_kernel(tc, xt, ht_minus_1, Wa, Wx, ba, bx, Lambda, out):
             chunk = list(range(first, first + n))
             first += n
             is_last = ci == len(CHUNKS) - 1
-            finish_per_step = -(-len(to_finish) // n)
             for i, g in enumerate(chunk):
-                ends_kernel = is_last and i == n - 1
-                count = 1 if ends_kernel else finish_per_step
+                count = 2 if i == 0 and len(to_finish) > n else 1
                 finishing, to_finish = to_finish[:count], to_finish[count:]
                 work = []
                 if i > 0:
@@ -382,7 +379,7 @@ def tile_cell_t_kernel(tc, xt, ht_minus_1, Wa, Wx, ba, bx, Lambda, out):
                     quantise_x(k)
                 if to_quantise and g > 1:
                     gpsimd_waits_for_codes(to_quantise[-1])
-                if to_multiply and not is_last:
+                if to_multiply and not (is_last and i > 0):
                     product(to_multiply.pop(0))
                 tanh_a(g, 0)
                 tanh_x(g, 0)

@@ -21,13 +21,19 @@ TILE = 4 * ROWS
 
 CHUNKS = (5, 5, 4, 2)
 
+START_NOW = (2, 3, 1)
+
 PREPARE = 2
 CODE_TILES = 11
+X_TILES = 5
 X_AHEAD = 3
 F_TILES = 4
+H_TILES = 3
 WARM_UP = 4
-
-START_NOW = (2, 3, 2)
+BANKS_BEFORE = 2
+BANKS_BETWEEN = 5
+PASSES_AT = 2
+GPSIMD_ROWS = 1
 
 
 def tile_cell_t_kernel(tc, xt, ht_minus_1, Wa, Wx, ba, bx, Lambda, out):
@@ -39,9 +45,9 @@ def tile_cell_t_kernel(tc, xt, ht_minus_1, Wa, Wx, ba, bx, Lambda, out):
 
     with ExitStack() as ctx:
         const = ctx.enter_context(tc.tile_pool(name="const", bufs=1))
-        xpool = ctx.enter_context(tc.tile_pool(name="xpool", bufs=5))
+        xpool = ctx.enter_context(tc.tile_pool(name="xpool", bufs=X_TILES))
         fpool = ctx.enter_context(tc.tile_pool(name="fpool", bufs=F_TILES))
-        hpool = ctx.enter_context(tc.tile_pool(name="hpool", bufs=3))
+        hpool = ctx.enter_context(tc.tile_pool(name="hpool", bufs=H_TILES))
         gpool = ctx.enter_context(tc.tile_pool(name="gpool", bufs=PREPARE))
         cpool = ctx.enter_context(tc.tile_pool(name="cpool", bufs=CODE_TILES))
         tapool = ctx.enter_context(tc.tile_pool(name="tapool", bufs=1))
@@ -205,6 +211,10 @@ def tile_cell_t_kernel(tc, xt, ht_minus_1, Wa, Wx, ba, bx, Lambda, out):
         def product(g):
             nc.gpsimd.tensor_tensor(out=ps[g][:], in0=ps[g][:], in1=a2s[g][:], op=ALU.mult)
 
+        def vector_product(g):
+            nc.vector.tensor_tensor(out=ps[g][:], in0=ps[g][:], in1=a2s[g][:], op=ALU.mult)
+            nc.gpsimd.tensor_copy(out=seen_product[:], in_=ps[g][:, TILE - 1:TILE])
+
         def product_rows(g, j, engine):
             io = rows_of(ps[g], j)
             engine.tensor_tensor(out=io, in0=io, in1=rows_of(qs[g], j), op=ALU.mult)
@@ -236,6 +246,7 @@ def tile_cell_t_kernel(tc, xt, ht_minus_1, Wa, Wx, ba, bx, Lambda, out):
         load_x(2)
 
         seen = const.tile([P, 1], U32, name="seen_codes")
+        seen_product = const.tile([P, 1], F32, name="seen_product")
         wcod, wsca = [], []
         for u in range(2):
             wcod.append(const.tile([P, D], U32, name="wcod%d" % u, align_bytes=64))
@@ -379,18 +390,20 @@ def tile_cell_t_kernel(tc, xt, ht_minus_1, Wa, Wx, ba, bx, Lambda, out):
                     quantise_x(k)
                 if to_quantise and g > 1:
                     gpsimd_waits_for_codes(to_quantise[-1])
+                if is_last and i == 0:
+                    vector_product(to_multiply.pop(0))
                 if to_multiply and not (is_last and i > 0):
                     product(to_multiply.pop(0))
                 tanh_a(g, 0)
                 tanh_x(g, 0)
                 if ci == 0 or i == 0:
-                    run_work(2)
+                    run_work(BANKS_BEFORE)
                 gate_passes(g, 0, 1)
                 gate_passes(g, 1, 1)
                 exp_a(g, 0)
                 tanh_a(g, 1)
                 tanh_x(g, 1)
-                run_work(4 if ci == 0 else 5)
+                run_work(BANKS_BETWEEN)
                 if i < n - 1:
                     gate_passes(g + 1, 0, 0)
                     gate_passes(g + 1, 1, 0)
@@ -411,7 +424,7 @@ def tile_cell_t_kernel(tc, xt, ht_minus_1, Wa, Wx, ba, bx, Lambda, out):
                 square_in_place(last)
                 for i, g in enumerate(chunk):
                     load_up_to("f", min(g + F_TILES - 1, last))
-                    if i == 2:
+                    if i == PASSES_AT:
                         gate_passes(last + 1, 0, 0)
                         gate_passes(last + 1, 1, 0)
                     sqrt(a2s[g][:])
@@ -441,13 +454,13 @@ def tile_cell_t_kernel(tc, xt, ht_minus_1, Wa, Wx, ba, bx, Lambda, out):
         for g in early:
             for j in range(4):
                 product_rows(g, j, nc.gpsimd)
-        for j in range(2):
+        for j in range(GPSIMD_ROWS):
             product_rows(last, j, nc.gpsimd)
         for g in early:
             for j in range(4):
                 finish(g, j)
                 store_rows(g, j)
-        for j in range(2, 4):
+        for j in range(GPSIMD_ROWS, 4):
             product_rows(last, j, nc.vector)
         for j in range(4):
             finish(last, j)

from contextlib import ExitStack

import concourse.mybir as mybir
from concourse.masks import make_identity

FLOPS = 2 * 2 * 8192 * 512 * 512

F32 = mybir.dt.float32
BF16 = mybir.dt.bfloat16
U32 = mybir.dt.uint32
U8 = mybir.dt.uint8
FP8X4 = mybir.dt.float8_e4m3fn_x4
ACT = mybir.ActivationFunctionType
ALU = mybir.AluOpType

P = 128
D = 512
ROWS = 512
GROUPS = 16
TILE = 4 * ROWS

CHUNKS = (5, 5, 4, 2)

START_NOW = (2, 3, 1)

PREPARE = 2
CODE_TILES = 11
X_TILES = 5
X_AHEAD = 3
F_TILES = 4
H_TILES = 3
WARM_UP = 4
BANKS_BEFORE = 2
BANKS_BETWEEN = 5
PASSES_AT = 2
GPSIMD_ROWS = 1


def tile_cell_t_kernel(tc, xt, ht_minus_1, Wa, Wx, ba, bx, Lambda, out):
    nc = tc.nc
    x_v = xt.rearrange("(g p j) k -> g p (j k)", p=P, j=4)
    h_v = ht_minus_1.rearrange("(g p j) k -> g p (j k)", p=P, j=4)
    o_v = out.rearrange("(g p j) k -> g p (j k)", p=P, j=4)
    o_rows = out.rearrange("(g p j) k -> g p j k", p=P, j=4)

    with ExitStack() as ctx:
        const = ctx.enter_context(tc.tile_pool(name="const", bufs=1))
        xpool = ctx.enter_context(tc.tile_pool(name="xpool", bufs=X_TILES))
        fpool = ctx.enter_context(tc.tile_pool(name="fpool", bufs=F_TILES))
        hpool = ctx.enter_context(tc.tile_pool(name="hpool", bufs=H_TILES))
        gpool = ctx.enter_context(tc.tile_pool(name="gpool", bufs=PREPARE))
        cpool = ctx.enter_context(tc.tile_pool(name="cpool", bufs=CODE_TILES))
        tapool = ctx.enter_context(tc.tile_pool(name="tapool", bufs=1))
        ppool = ctx.enter_context(tc.tile_pool(name="ppool", bufs=max(CHUNKS) + 1))
        apool = ctx.enter_context(tc.tile_pool(name="apool", bufs=max(CHUNKS)))
        rpool = ctx.enter_context(tc.tile_pool(name="rpool", bufs=max(CHUNKS) + 1))
        psum = ctx.enter_context(tc.psum_pool(name="psum", bufs=1))
        ctx.enter_context(tc.manual_schedule())

        banks_used = [0]

        def transpose_bank():
            i = banks_used[0]
            banks_used[0] = i + 1
            return psum.tile([P, 512], F32, tag="T%d" % (i % 4), name="T_%d" % i)

        def gate_bank(i, name):
            return psum.tile([P, 512], F32, tag="Z%d" % i, name=name)

        xs, fs, hs, grouped, codes, scales, zs = {}, {}, {}, {}, {}, {}, {}
        tas, ps, a2s, qs, rs = {}, {}, {}, {}, {}

        def load_x(g):
            xs[g] = xpool.tile([P, TILE], BF16, tag="x", name="x%d" % g)
            nc.sync.dma_start(out=xs[g][:], in_=x_v[g])

        def load_f(g):
            fs[g] = fpool.tile([P, TILE], BF16, tag="f", name="f%d" % g)
            nc.sync.dma_start(out=fs[g][:], in_=x_v[g])

        def load_h(g):
            hs[g] = hpool.tile([P, TILE], BF16, tag="h", name="h%d" % g)
            nc.sync.dma_start(out=hs[g][:], in_=h_v[g])

        def load_w(u):
            t = xpool.tile([P, TILE], BF16, tag="x", name="w_sb%d" % u)
            for gate, w in enumerate((Wa, Wx)):
                nc.sync.dma_start(out=t[:, gate * 1024:(gate + 1) * 1024],
                                  in_=w[256 * u:256 * (u + 1), :].rearrange("(m e) k -> m (e k)", e=2))
            return t

        def mx_transposes(src, half):
            words = src[:].bitcast(F32)
            bank = transpose_bank()
            for jl in range(2):
                row = (2 * half + jl) * 256
                for u in range(2):
                    col = u * 256 + jl * P
                    nc.tensor.transpose(bank[:, col:col + P], words[:, row + u:row + 256:2], ident[:])
            return bank

        def regroup(bank, grp, half, copy=nc.vector.tensor_copy):
            copy(out=grp[:, half * 512:(half + 1) * 512].rearrange("p (c u) -> p c u", u=2),
                 in_=bank[:].rearrange("p (u c) -> p c u", u=2))

        def new_grouped(name):
            return gpool.tile([P, TILE // 2], F32, tag="grp", name="grp_" + name, align_bytes=64)

        def quantise(grp, cod, sca, lo=0, hi=ROWS):
            nc.vector.quantize_mx(out=cod[:, lo:hi].bitcast(FP8X4), scales=sca[:, lo:hi],
                                  in_=grp[:, 2 * lo:2 * hi].bitcast(BF16))

        def prepare_x(g, half):
            if half == 0:
                grouped[g] = new_grouped("x%d" % g)
            regroup(mx_transposes(xs[g], half), grouped[g], half)

        def quantise_x(g):
            codes[g] = cpool.tile([P, ROWS], U32, tag="cod", name="cod%d" % g, align_bytes=64)
            scales[g] = cpool.tile([P, ROWS], U8, tag="sca", name="sca%d" % g, align_bytes=64)
            quantise(grouped[g], codes[g], scales[g])

        def gpsimd_waits_for_codes(g):
            nc.gpsimd.tensor_copy(out=seen[:], in_=codes[g][:, 0:1])

        def gate_passes(g, gate, u):
            for e in range(2):
                col = (2 * gate + e) * P
                z = gate_bank(2 * gate + e, "z%d_%d_%d" % (gate, g, 2 * u + e))
                nc.tensor.matmul_mx(
                    out=z[:],
                    lhsT=wcod[u][:, col:col + P].bitcast(FP8X4),
                    lhsT_scale=wsca[u][:, col:col + P],
                    rhs=codes[g][:].bitcast(FP8X4),
                    rhs_scale=scales[g][:],
                    start=True, stop=True)
                zs[(g, gate, 2 * u + e)] = z

        def tanh_a(g, u):
            if u == 0:
                tas[g] = tapool.tile([P, TILE], F32, tag="ta", name="ta%d" % g)
            for b in (2 * u, 2 * u + 1):
                nc.scalar.activation(out=tas[g][:, b * ROWS:(b + 1) * ROWS], in_=zs[(g, 0, b)][:],
                                     func=ACT.Tanh, scale=0.5, bias=half_bias[:, b:b + 1])

        def tanh_x(g, u):
            if u == 0:
                ps[g] = ppool.tile([P, TILE], F32, tag="p", name="p%d" % g)
            for b in (2 * u, 2 * u + 1):
                nc.scalar.activation(out=ps[g][:, b * ROWS:(b + 1) * ROWS], in_=zs[(g, 1, b)][:],
                                     func=ACT.Tanh, scale=0.5, bias=half_bias[:, 4 + b:5 + b])

        def exp_a(g, u):
            if u == 0:
                a2s[g] = apool.tile([P, TILE], F32, tag="a2", name="a2_%d" % g)
            for b in (2 * u, 2 * u + 1):
                nc.scalar.activation(out=a2s[g][:, b * ROWS:(b + 1) * ROWS],
                                     in_=tas[g][:, b * ROWS:(b + 1) * ROWS],
                                     func=ACT.Exp, scale=nc4[:, b:b + 1], bias=nc4[:, b:b + 1])

        def sqrt(ap):
            nc.scalar.activation(out=ap, in_=ap, func=ACT.Sqrt, scale=-0.25, bias=quarter[:])

        def rows_of(t, j):
            return t[:].rearrange("p (b n) -> p b n", b=4)[:, :, j * P:(j + 1) * P]

        def back_transposes(src, j):
            bank = transpose_bank()
            for b in range(4):
                nc.tensor.transpose(bank[:, b * P:(b + 1) * P],
                                    src[:, b * ROWS + j * P:b * ROWS + (j + 1) * P], ident[:])
            return bank[:].rearrange("p (u e m) -> p u m e", u=2, e=2)

        def row(t, j):
            return t[:, j * D:(j + 1) * D].rearrange("p (u m e) -> p u m e", u=2, e=2)

        def times_h(g, j):
            if j == 0:
                rs[g] = rpool.tile([P, TILE], F32, tag="r", name="r%d" % g)
            nc.vector.tensor_tensor(out=row(rs[g], j), in0=back_transposes(a2s[g], j), in1=row(hs[g], j),
                                    op=ALU.mult)

        def finish(g, j):
            nc.vector.tensor_tensor(out=row(rs[g], j), in0=back_transposes(ps[g], j), in1=row(rs[g], j),
                                    op=ALU.add)

        def times_x(g, half):
            words = fs[g][:].bitcast(F32)
            bank = transpose_bank()
            for jl in range(2):
                for u in range(2):
                    col = (2 * half + jl) * 256 + u * P
                    nc.tensor.transpose(bank[:, u * 256 + jl * P:u * 256 + (jl + 1) * P],
                                        words[:, col:col + P], ident[:])
            x_bf = bank[:].bitcast(BF16)
            blocks = ps[g][:].rearrange("p (b n) -> p b n", b=4)
            for u in range(2):
                io = blocks[:, 2 * u:2 * u + 2, half * 256:(half + 1) * 256]
                nc.vector.scalar_tensor_tensor(
                    out=io, in0=io, scalar=1.0,
                    in1=x_bf[:, u * 512:(u + 1) * 512].rearrange("p (c e) -> p e c", e=2),
                    op0=ALU.add, op1=ALU.mult)

        def square_in_place(g):
            nc.gpsimd.tensor_tensor(out=a2s[g][:], in0=a2s[g][:], in1=a2s[g][:], op=ALU.mult)

        def new_squares(g):
            qs[g] = apool.tile([P, TILE], F32, tag="a2", name="q%d" % g)
            return qs[g]

        def product(g):
            nc.gpsimd.tensor_tensor(out=ps[g][:], in0=ps[g][:], in1=a2s[g][:], op=ALU.mult)

        def vector_product(g):
            nc.vector.tensor_tensor(out=ps[g][:], in0=ps[g][:], in1=a2s[g][:], op=ALU.mult)
            nc.gpsimd.tensor_copy(out=seen_product[:], in_=ps[g][:, TILE - 1:TILE])

        def product_rows(g, j, engine):
            io = rows_of(ps[g], j)
            engine.tensor_tensor(out=io, in0=io, in1=rows_of(qs[g], j), op=ALU.mult)

        def store(g):
            nc.sync.dma_start(out=o_v[g], in_=rs[g][:])

        def store_rows(g, j):
            nc.sync.dma_start(out=o_rows[g][:, j, :], in_=rs[g][:, j * D:(j + 1) * D])

        zeros = const.tile([P, 512], BF16, name="zeros")
        nc.gpsimd.memset(zeros[:].bitcast(U32), 0)
        vectors = const.tile([P, P], F32, name="vt")
        nc.gpsimd.memset(vectors[:], 0.0)
        ident = const.tile([P, P], F32, name="ident")
        make_identity(nc, ident[:])
        quarter = const.tile([P, 1], F32, name="quarter")
        nc.vector.memset(quarter[:], 0.25)
        for v, vec in enumerate((ba, bx, Lambda)):
            nc.scalar.dma_start(out=vectors[:].bitcast(BF16)[2 * v:2 * v + 2, :],
                                in_=vec.rearrange("o (u w) -> (o u) w", u=2))

        xs[0] = xpool.tile([P, TILE], BF16, tag="x", name="x0")
        for half in range(2):
            cols = slice(half * 1024, (half + 1) * 1024)
            nc.sync.dma_start(out=xs[0][:, cols], in_=x_v[0][:, cols])
        w_sb = [load_w(0), load_w(1)]
        load_x(1)
        load_x(2)

        seen = const.tile([P, 1], U32, name="seen_codes")
        seen_product = const.tile([P, 1], F32, name="seen_product")
        wcod, wsca = [], []
        for u in range(2):
            wcod.append(const.tile([P, D], U32, name="wcod%d" % u, align_bytes=64))
            wsca.append(const.tile([P, D], U8, name="wsca%d" % u, align_bytes=64))

        for i in range(WARM_UP):
            z = gate_bank(i % 4, "warm_up%d" % i)
            nc.tensor.matmul(z[:], lhsT=zeros[:, 0:P], rhs=zeros[:], start=True, stop=True)
        grouped[0] = new_grouped("x0")
        x0_banks = [mx_transposes(xs[0], 0), mx_transposes(xs[0], 1)]
        load_x(3)
        load_h(0)
        vector_bank = transpose_bank()
        nc.tensor.transpose(vector_bank[:, 0:P], vectors[:], ident[:])
        vec_bf = vector_bank[:].bitcast(BF16)
        w0_banks = [mx_transposes(w_sb[0], 0)]

        e_abs = const.tile([P, 4], F32, name="e_abs")
        nc.scalar.activation(out=e_abs[:], in_=vec_bf[:, 8:12], func=ACT.Abs)
        e_neg = const.tile([P, 4], F32, name="e_neg")
        nc.scalar.activation(out=e_neg[:], in_=e_abs[:], func=ACT.Exp, scale=-1.0)

        regroup(x0_banks[0], grouped[0], 0)
        regroup(x0_banks[1], grouped[0], 1)
        quantise_x(0)
        raw = const.tile([P, 12], F32, name="raw")
        nc.vector.tensor_copy(out=raw[:], in_=vec_bf[:, 0:12])
        half_bias = const.tile([P, 8], F32, name="hb")
        nc.vector.tensor_scalar_mul(out=half_bias[:], in0=raw[:, 0:8], scalar1=0.5)

        lam4, den, inv, z1, z2, z4, odd, even, art, nc4 = [
            const.tile([P, 4], F32, name=name)
            for name in ("lam4", "den", "inv", "z1", "z2", "z4", "odd", "even", "art", "nc4")]

        def horner(acc, n):
            return lambda: nc.vector.scalar_tensor_tensor(
                out=acc[:], in0=acc[:], scalar=1.0 / n, in1=z4[:], op0=ALU.add, op1=ALU.mult)

        series = [
            lambda: nc.vector.tensor_scalar(out=lam4[:], in0=raw[:, 8:12], scalar1=0.0, scalar2=-4.0,
                                            op0=ALU.max, op1=ALU.mult),
            lambda: nc.vector.tensor_scalar_add(out=den[:], in0=e_neg[:], scalar1=2.0),
            lambda: nc.vector.reciprocal(out=inv[:], in_=den[:]),
            lambda: nc.vector.tensor_tensor(out=z1[:], in0=e_neg[:], in1=inv[:], op=ALU.mult),
            lambda: nc.vector.tensor_tensor(out=z2[:], in0=z1[:], in1=z1[:], op=ALU.mult),
            lambda: nc.vector.tensor_tensor(out=z4[:], in0=z2[:], in1=z2[:], op=ALU.mult),
            lambda: nc.vector.tensor_scalar_mul(out=odd[:], in0=z4[:], scalar1=1.0 / 19.0),
            lambda: nc.vector.tensor_scalar_mul(out=even[:], in0=z4[:], scalar1=1.0 / 17.0),
            horner(odd, 15), horner(even, 13), horner(odd, 11), horner(even, 9), horner(odd, 7),
            lambda: nc.vector.scalar_tensor_tensor(out=even[:], in0=even[:], scalar=1.0 / 5.0, in1=z2[:],
                                                   op0=ALU.add, op1=ALU.mult),
            lambda: nc.vector.scalar_tensor_tensor(out=odd[:], in0=odd[:], scalar=1.0 / 3.0, in1=even[:],
                                                   op0=ALU.add, op1=ALU.add),
            lambda: nc.vector.tensor_tensor(out=odd[:], in0=odd[:], in1=z2[:], op=ALU.mult),
            lambda: nc.vector.scalar_tensor_tensor(out=art[:], in0=odd[:], scalar=1.0, in1=z1[:],
                                                   op0=ALU.add, op1=ALU.mult),
            lambda: nc.vector.scalar_tensor_tensor(out=nc4[:], in0=art[:], scalar=-8.0, in1=lam4[:],
                                                   op0=ALU.mult, op1=ALU.add),
        ]

        def run_series(count):
            for i in range(count):
                series.pop(0)()

        w_grouped = [new_grouped("w0")]
        regroup(w0_banks[0], w_grouped[0], 0, nc.scalar.copy)
        run_series(3)
        quantise(w_grouped[0], wcod[0], wsca[0], 0, 256)
        run_series(1)
        w0_banks.append(mx_transposes(w_sb[0], 1))
        w1_banks = [mx_transposes(w_sb[1], 0)]
        load_x(4)
        load_h(1)
        regroup(w0_banks[1], w_grouped[0], 1, nc.scalar.copy)
        run_series(1)
        quantise(w_grouped[0], wcod[0], wsca[0], 256, 512)
        run_series(1)
        w_grouped.append(new_grouped("w1"))
        regroup(w1_banks[0], w_grouped[1], 0, nc.scalar.copy)
        gate_passes(0, 0, 0)
        gate_passes(0, 1, 0)
        w1_banks.append(mx_transposes(w_sb[1], 1))
        run_series(9)
        regroup(w1_banks[1], w_grouped[1], 1)
        run_series(len(series))
        quantise(w_grouped[1], wcod[1], wsca[1])
        prepare_x(1, 0)
        prepare_x(1, 1)

        loaders = {"x": load_x, "h": load_h, "f": load_f}
        loaded = {"x": 5, "h": 2, "f": 0}

        def load_up_to(kind, g):
            while loaded[kind] < GROUPS and loaded[kind] <= g:
                loaders[kind](loaded[kind])
                loaded[kind] += 1

        prepared = 1
        to_quantise = [1]
        to_multiply = []
        to_finish = []
        first = 0
        for ci, n in enumerate(CHUNKS):
            chunk = list(range(first, first + n))
            first += n
            is_last = ci == len(CHUNKS) - 1
            for i, g in enumerate(chunk):
                count = 2 if i == 0 and len(to_finish) > n else 1
                finishing, to_finish = to_finish[:count], to_finish[count:]
                work = []
                if i > 0:
                    work.extend([(times_h, g - 1, j) for j in range(4)])
                for done in finishing:
                    work.extend([(finish, done, j) for j in range(4)])
                if is_last and i < n - 1:
                    work.extend([(times_x, g, 0), (times_x, g, 1)])
                if ci == 0 or i == 0:
                    for k in range(prepared + 1, min(prepared + 1 + PREPARE, GROUPS)):
                        work.extend([(prepare_x, k, 0), (prepare_x, k, 1)])
                        prepared = k
                load_up_to("x", prepared + X_AHEAD)
                load_up_to("h", g + 1)
                load_up_to("f", g if is_last else g - 1 if i > 0 else -1)
                new_codes = []

                def run_work(count):
                    for what, group, part in work[:count]:
                        if is_last and what is times_h and part == 0:
                            squares = new_squares(group)
                            nc.gpsimd.tensor_tensor(out=squares[:], in0=a2s[group][:], in1=a2s[group][:],
                                                    op=ALU.mult)
                            product(to_multiply.pop(0))
                        what(group, part)
                        if what is times_h and part == 3 and not is_last:
                            square_in_place(group)
                        if what is prepare_x and part == 1:
                            new_codes.append(group)
                    work[:count] = []

                for k in to_quantise:
                    quantise_x(k)
                if to_quantise and g > 1:
                    gpsimd_waits_for_codes(to_quantise[-1])
                if is_last and i == 0:
                    vector_product(to_multiply.pop(0))
                if to_multiply and not (is_last and i > 0):
                    product(to_multiply.pop(0))
                tanh_a(g, 0)
                tanh_x(g, 0)
                if ci == 0 or i == 0:
                    run_work(BANKS_BEFORE)
                gate_passes(g, 0, 1)
                gate_passes(g, 1, 1)
                exp_a(g, 0)
                tanh_a(g, 1)
                tanh_x(g, 1)
                run_work(BANKS_BETWEEN)
                if i < n - 1:
                    gate_passes(g + 1, 0, 0)
                    gate_passes(g + 1, 1, 0)
                exp_a(g, 1)
                run_work(len(work))
                to_quantise = new_codes
                for done in finishing:
                    store(done)

            last = chunk[-1]
            if not is_last:
                for k in to_quantise:
                    quantise_x(k)
                    gpsimd_waits_for_codes(k)
                to_quantise = []
                for j in range(4):
                    times_h(last, j)
                square_in_place(last)
                for i, g in enumerate(chunk):
                    load_up_to("f", min(g + F_TILES - 1, last))
                    if i == PASSES_AT:
                        gate_passes(last + 1, 0, 0)
                        gate_passes(last + 1, 1, 0)
                    sqrt(a2s[g][:])
                    times_x(g, 0)
                    times_x(g, 1)
                    if i < START_NOW[ci]:
                        product(g)
                    else:
                        to_multiply.append(g)
                to_finish = to_finish + chunk

        early, last = chunk[:-1], chunk[-1]
        for g in early:
            for j in range(4):
                sqrt(rows_of(qs[g], j))
        nc.scalar.activation(out=new_squares(last)[:], in_=a2s[last][:], func=ACT.Square)
        for j in range(4):
            sqrt(rows_of(qs[last], j))
        for j in range(4):
            times_h(last, j)
        times_x(last, 0)
        times_x(last, 1)
        for g in to_finish:
            for j in range(4):
                finish(g, j)
            store(g)
        for g in early:
            for j in range(4):
                product_rows(g, j, nc.gpsimd)
        for j in range(GPSIMD_ROWS):
            product_rows(last, j, nc.gpsimd)
        for g in early:
            for j in range(4):
                finish(g, j)
                store_rows(g, j)
        for j in range(GPSIMD_ROWS, 4):
            product_rows(last, j, nc.vector)
        for j in range(4):
            finish(last, j)
            store_rows(last, j)
